import numpy as np
import ml_dtypes


def mxq(x, axis, fmt="e4m3"):
    dtype, down = {"e4m3": (ml_dtypes.float8_e4m3fn, 7), "e5m2": (ml_dtypes.float8_e5m2, 14)}[fmt]
    v = np.moveaxis(np.asarray(x, np.float32).astype(ml_dtypes.bfloat16).astype(np.float64), axis, -1)
    blocks = v.reshape(v.shape[:-1] + (-1, 32))
    amax = np.abs(blocks).max(-1, keepdims=True)
    byte = np.maximum(np.where(amax > 0, np.frexp(amax)[1] - 1 + 127, 0) - down, 1)
    scale = np.exp2(byte - 127.0)
    codes = (blocks / scale).astype(np.float32).astype(dtype).astype(np.float64)
    return np.moveaxis((codes * scale).reshape(v.shape), -1, axis)


WIDE = False


def mx_kscale(k):
    if not WIDE:
        return np.ones(k)
    levels = np.array([10, -10, 5, -5, 0])
    if k % 512:
        return np.exp2(np.random.permutation(np.resize(levels, k // 32))).repeat(32)
    a = np.empty((k // 512, 16))
    for p in range(k // 512):
        a[p, :8] = np.random.permutation(np.resize(levels, 8))
        for g in range(8):
            far = levels[np.abs(levels - a[p, g]) >= 10]
            a[p, g + 8] = far[np.random.randint(len(far))]
    return np.exp2(a.ravel()).repeat(32)


BF16 = ml_dtypes.bfloat16


def bf(x):
    return np.asarray(x, np.float32).astype(BF16)


def f64(x):
    return np.asarray(x).astype(np.float64)


B, N, DIN, DH, DOUT = 1536, 4, 512, 512, 512
EPS = 1e-5


def elu(v):
    return np.where(v > 0.0, v, np.expm1(np.minimum(v, 0.0)))


def sigmoid(v):
    return 1.0 / (1.0 + np.exp(-v))


def setup_inputs():
    rn = np.random.standard_normal
    s, t = mx_kscale(DH), mx_kscale(DOUT)
    z = rn((B, N, DOUT))
    e = np.exp(z - z.max(1, keepdims=True))
    return {
        "hv": bf(elu(rn((B, N, DH))) * s),
        "x": bf(rn((B, N, DIN)) + 0.5),
        "sel_w": bf(e / e.sum(1, keepdims=True)),
        "vW1": bf(rn((N, DH, DOUT)) * 1.2 / np.sqrt(DH) / s[:, None] * t),
        "vb1": bf(rn((N, DOUT)) * 0.3 * t),
        "vW4": bf(rn((N, DOUT, DOUT)) / np.sqrt(DOUT) / t[:, None]),
        "vb4": bf(rn((N, DOUT)) * 0.3),
        "vW5": bf(rn((N, DOUT, DOUT)) / np.sqrt(DOUT) / t[:, None]),
        "vb5": bf(rn((N, DOUT)) * 0.3),
        "vlng": bf(1.0 + 0.2 * rn((N, DOUT))),
        "vlnb": bf(0.2 * rn((N, DOUT))),
    }


def reference(hv, x, sel_w, vW1, vb1, vW4, vb4, vW5, vb5, vlng, vlnb):
    hq = mxq(f64(hv).transpose(1, 0, 2), 2, "e4m3")
    e1v = (hq @ mxq(f64(vW1), 1, "e4m3")) + f64(vb1)[:, None, :]
    eq = mxq(e1v, 2, "e4m3")
    gv = sigmoid((eq @ mxq(f64(vW4), 1, "e4m3")) + f64(vb4)[:, None, :]) * ((eq @ mxq(f64(vW5), 1, "e4m3")) + f64(vb5)[:, None, :])
    r = f64(x) + gv.transpose(1, 0, 2)
    yv = (r - r.mean(-1, keepdims=True)) * (1.0 / np.sqrt(r.var(-1, keepdims=True) + EPS)) * f64(vlng) + f64(vlnb)
    return np.sum(f64(sel_w) * yv, axis=1)

@@ -1,0 +1,375 @@
+from contextlib import ExitStack
+
+import concourse.mybir as mybir
+from concourse.masks import make_identity
+
+F32 = mybir.dt.float32
+BF16 = mybir.dt.bfloat16
+U32 = mybir.dt.uint32
+U8 = mybir.dt.uint8
+FP8X4 = mybir.dt.float8_e4m3fn_x4
+ALU = mybir.AluOpType
+ACT = mybir.ActivationFunctionType
+
+P = 128
+PACK = 4
+BATCH = 1536
+VARS = 4
+D = 512
+CHUNKS = D // P
+UNIT_ROWS = 512
+UNIT_TILES = UNIT_ROWS // P
+UNITS = BATCH // UNIT_ROWS
+TOTAL = VARS * UNITS
+EPS = 1e-5
+
+FLOPS = 3 * VARS * 2 * BATCH * D * D
+
+
+def tile_variableselectionnetwork_pb_t_kernel(
+    tc, hv, x, sel_w, vW1, vb1, vW4, vb4, vW5, vb5, vlng, vlnb, out
+):
+    nc = tc.nc
+    with ExitStack() as ctx:
+        ctx.enter_context(tc.manual_schedule())
+        const = ctx.enter_context(tc.tile_pool(name="const", bufs=1))
+        wstage = ctx.enter_context(tc.tile_pool(name="wstage", bufs=2))
+        wquant = ctx.enter_context(tc.tile_pool(name="wquant", bufs=VARS))
+        loads = ctx.enter_context(tc.tile_pool(name="loads", bufs=4))
+        quant = ctx.enter_context(tc.tile_pool(name="quant", bufs=2))
+        gate = ctx.enter_context(tc.tile_pool(name="gate", bufs=2))
+        norm = ctx.enter_context(tc.tile_pool(name="norm", bufs=2 * UNIT_TILES))
+        stat = ctx.enter_context(tc.tile_pool(name="stat", bufs=3))
+        psum = ctx.enter_context(tc.psum_pool(name="psum", bufs=4))
+
+        ident_f = const.tile([P, P], F32)
+        make_identity(nc, ident_f[:])
+        ident_b = const.tile([P, P], BF16)
+        make_identity(nc, ident_b[:])
+        neg_half = const.tile([P, UNIT_TILES], F32)
+        nc.vector.memset(neg_half[:], -0.5)
+
+        vb1_cols = const.tile([P, VARS, CHUNKS], BF16)
+        nc.scalar.dma_start(out=vb1_cols[:], in_=vb1.rearrange("n (p c) -> p n c", c=CHUNKS))
+        bias_rows = const.tile([P, P], BF16)
+        nc.vector.memset(bias_rows[:], 0.0)
+        for k, vec in enumerate((vb4, vb5)):
+            nc.scalar.dma_start(
+                out=bias_rows[k * VARS * CHUNKS : (k + 1) * VARS * CHUNKS, :],
+                in_=vec.rearrange("n (c m) -> (n c) m", m=P),
+            )
+        gs_rows = const.tile([P, D], BF16)
+        nc.vector.memset(gs_rows[:], 0.0)
+        nc.scalar.dma_start(out=gs_rows[0:VARS, :], in_=vlng)
+        nc.scalar.dma_start(out=gs_rows[VARS : 2 * VARS, :], in_=vlnb)
+
+        bias_ps = psum.tile([P, P], BF16, tag="to_scalar")
+        nc.tensor.transpose(bias_ps[:], bias_rows[:], ident_b[:])
+        bias_cols = const.tile([P, 2, VARS, CHUNKS], F32)
+        nc.scalar.copy(
+            out=bias_cols[:].rearrange("p k n c -> p (k n c)"), in_=bias_ps[:, 0 : 2 * VARS * CHUNKS]
+        )
+
+
+        acc = const.tile([P, BATCH // P, D], F32)
+
+        tiles = {}
+
+        def live(k):
+            return 0 <= k < TOTAL
+
+        def weight_load(m):
+            n = m // 3
+            raw = wstage.tile([P, PACK, D], BF16, tag="w_raw", bufs=4)
+            w = (vW1, vW4, vW5)[m % 3]
+            nc.sync.dma_start(out=raw[:], in_=w[n].rearrange("(p t) c -> p t c", t=PACK))
+            tiles["w_raw", m] = raw
+
+        def weight_regroup(m):
+            raw = tiles["w_raw", m]
+            grouped = wstage.tile([P, D, PACK], BF16, tag="w_grp", align_bytes=64)
+            tiles["w_grp", m] = grouped
+            if m % 3 == 0:
+                permuted = grouped[:].rearrange("p (t m) j -> p t m j", t=PACK)
+                by_chunk = raw[:].rearrange("p j (m t) -> p t m j", t=PACK)
+                nc.vector.tensor_copy(out=permuted[:, 0:2], in_=by_chunk[:, 0:2])
+                nc.scalar.copy(out=permuted[:, 2:4], in_=by_chunk[:, 2:4])
+                return
+            nc.vector.tensor_copy(
+                out=grouped[:, 0:320, :].rearrange("p (c i) t -> p c t i", i=4),
+                in_=raw[:, :, 0:320].rearrange("p t (c i) -> p c t i", i=4),
+            )
+            nc.scalar.copy(
+                out=grouped[:, 320:D, :].rearrange("p (c i) t -> p c t i", i=4),
+                in_=raw[:, :, 320:D].rearrange("p t (c i) -> p c t i", i=4),
+            )
+
+        def weight_quantise(m):
+            codes = wquant.tile([P, D], U32, tag="w_codes%d" % (m % 3), align_bytes=64)
+            scales = wquant.tile([P, D], U8, tag="w_scales%d" % (m % 3), align_bytes=64)
+            nc.vector.quantize_mx(
+                out=codes[:].bitcast(FP8X4),
+                scales=scales[:],
+                in_=tiles["w_grp", m][:].rearrange("p c t -> p (c t)"),
+            )
+            tiles["w_codes", m] = codes
+            tiles["w_scales", m] = scales
+
+        def mx_pass(out_ps, m, c, codes, scales):
+            feats = slice(c * P, (c + 1) * P)
+            nc.tensor.matmul_mx(
+                out=out_ps,
+                lhsT=tiles["w_codes", m][:, feats].bitcast(FP8X4),
+                lhsT_scale=tiles["w_scales", m][:, feats],
+                rhs=codes[:].bitcast(FP8X4),
+                rhs_scale=scales[:],
+                start=True,
+                stop=True,
+            )
+
+        def unit_rows(dram, k):
+            first = (k % UNITS) * UNIT_ROWS
+            return dram[first : first + UNIT_ROWS, k // UNITS, :].rearrange("(i p) d -> p i d", p=P)
+
+        def load_hv(k):
+            hv_u = loads.tile([P, UNIT_TILES * D], BF16, tag="hv_u")
+            nc.sync.dma_start(out=hv_u[:].rearrange("p (i d) -> p i d", i=UNIT_TILES), in_=unit_rows(hv, k))
+            tiles["hv_u", k] = hv_u
+
+        def load_x_sel(k):
+            x_u = loads.tile([P, UNIT_TILES, D], BF16, tag="x_u", bufs=3)
+            nc.sync.dma_start(out=x_u[:], in_=unit_rows(x, k))
+            sel_u = loads.tile([P, UNIT_TILES, D], BF16, tag="sel_u")
+            nc.sync.dma_start(out=sel_u[:], in_=unit_rows(sel_w, k))
+            tiles["x_u", k] = x_u
+            tiles["sel_u", k] = sel_u
+
+        def hv_transpose(k, half):
+            hv_words = tiles["hv_u", k][:].bitcast(F32)
+            if half == 0:
+                hv_grp = quant.tile([P, UNIT_ROWS * PACK], BF16, tag="hv_grp", align_bytes=64)
+            else:
+                hv_grp = tiles["hv_grp", k]
+            hv_grp_words = hv_grp[:].bitcast(F32).rearrange("p (b u) -> p b u", u=2)
+            if True:
+                hv_t = psum.tile([P, 2, 2 * P], F32, tag="to_scalar")
+                for u in range(2):
+                    for j in range(2):
+                        i = 2 * half + j
+                        nc.tensor.transpose(
+                            hv_t[:, u, j * P : (j + 1) * P],
+                            hv_words[:, i * 2 * P + u : (i + 1) * 2 * P : 2],
+                            ident_f[:],
+                        )
+                nc.scalar.copy(
+                    out=hv_grp_words[:, half * 2 * P : (half + 1) * 2 * P, :],
+                    in_=hv_t[:].rearrange("p u b -> p b u"),
+                )
+            tiles["hv_grp", k] = hv_grp
+
+        def hv_quantise(k):
+            codes = quant.tile([P, UNIT_ROWS], U32, tag="hv_codes", align_bytes=64)
+            scales = quant.tile([P, UNIT_ROWS], U8, tag="hv_scales", align_bytes=64)
+            nc.vector.quantize_mx(out=codes[:].bitcast(FP8X4), scales=scales[:], in_=tiles["hv_grp", k][:])
+            tiles["hv_codes", k] = codes
+            tiles["hv_scales", k] = scales
+
+        def first_layer(k):
+            n = k // UNITS
+            planes = quant.tile([P, CHUNKS, UNIT_ROWS], BF16, tag="e1_planes")
+            for c in range(CHUNKS):
+                e1_ps = psum.tile([P, UNIT_ROWS], F32, tag="to_scalar")
+                mx_pass(e1_ps[:], 3 * n, c, tiles["hv_codes", k], tiles["hv_scales", k])
+                nc.scalar.activation(
+                    out=planes[:, c, :], in_=e1_ps[:], func=ACT.Identity, bias=vb1_cols[:, n, c : c + 1], scale=1.0
+                )
+            tiles["e1_planes", k] = planes
+
+        def e1_regroup(k):
+            grouped = quant.tile([P, UNIT_ROWS, PACK], BF16, tag="e1_grp", align_bytes=64)
+            nc.vector.tensor_copy(
+                out=grouped[:].rearrange("p (b i) t -> p b t i", i=4),
+                in_=tiles["e1_planes", k][:].rearrange("p t (b i) -> p b t i", i=4),
+            )
+            tiles["e1_grp", k] = grouped
+
+        def e1_quantise(k):
+            codes = quant.tile([P, UNIT_ROWS], U32, tag="e1_codes", align_bytes=64)
+            scales = quant.tile([P, UNIT_ROWS], U8, tag="e1_scales", align_bytes=64)
+            nc.vector.quantize_mx(
+                out=codes[:].bitcast(FP8X4),
+                scales=scales[:],
+                in_=tiles["e1_grp", k][:].rearrange("p b t -> p (b t)"),
+            )
+            tiles["e1_codes", k] = codes
+            tiles["e1_scales", k] = scales
+
+        def gate_layers(k):
+            n = k // UNITS
+            gv_t = gate.tile([P, CHUNKS, UNIT_ROWS], F32, tag="gv_t")
+            for c in range(CHUNKS):
+                g4_ps = psum.tile([P, UNIT_ROWS], F32, tag="to_scalar")
+                mx_pass(g4_ps[:], 3 * n + 1, c, tiles["e1_codes", k], tiles["e1_scales", k])
+                g5_ps = psum.tile([P, UNIT_ROWS], F32, tag="to_vector", bufs=3)
+                mx_pass(g5_ps[:], 3 * n + 2, c, tiles["e1_codes", k], tiles["e1_scales", k])
+                sig = gate.tile([P, UNIT_ROWS], F32, tag="sig", bufs=3)
+                nc.scalar.activation(
+                    out=sig[:], in_=g4_ps[:], func=ACT.Sigmoid, bias=bias_cols[:, 0, n, c : c + 1], scale=1.0
+                )
+                nc.vector.scalar_tensor_tensor(
+                    out=gv_t[:, c, :],
+                    in0=g5_ps[:],
+                    scalar=bias_cols[:, 1, n, c : c + 1],
+                    in1=sig[:],
+                    op0=ALU.add,
+                    op1=ALU.mult,
+                )
+            tiles["gv_t", k] = gv_t
+
+        def residual(k):
+            row_sum = stat.tile([P, UNIT_TILES], F32, tag="row_sum")
+            for i in range(UNIT_TILES):
+                r_ps = psum.tile([P, D], F32, tag="to_scalar")
+                nc.tensor.matmul(out=r_ps[:], lhsT=ident_b[:], rhs=tiles["x_u", k][:, i, :], start=True, stop=False)
+                for c in range(CHUNKS):
+                    nc.tensor.matmul(
+                        out=r_ps[:, c * P : (c + 1) * P],
+                        lhsT=tiles["gv_t", k][:, c, i * P : (i + 1) * P],
+                        rhs=ident_f[:],
+                        is_transpose=True,
+                        start=False,
+                        stop=(c == CHUNKS - 1),
+                    )
+                r = norm.tile([P, D], F32, tag="r")
+                nc.scalar.activation(out=r[:], in_=r_ps[:], func=ACT.Identity, accum_out=row_sum[:, i : i + 1])
+                tiles["r%d" % i, k] = r
+            tiles["row_sum", k] = row_sum
+
+        def mean(k):
+            neg_mean = stat.tile([P, UNIT_TILES], F32, tag="neg_mean")
+            nc.scalar.mul(out=neg_mean[:], in_=tiles["row_sum", k][:], mul=-1.0 / D)
+            tiles["neg_mean", k] = neg_mean
+
+        def spread_gain_shift(n):
+            gs_ps = psum.tile([P, 2, D], BF16, tag="gain_shift", bufs=1)
+            for v in range(2):
+                row = v * VARS + n
+                nc.tensor.matmul(
+                    out=gs_ps[:, v, :],
+                    lhsT=ident_b[:, row : row + 1].to_broadcast([P, P]),
+                    rhs=gs_rows[:],
+                    start=True,
+                    stop=True,
+                )
+            tiles["gain_shift", n] = gs_ps
+
+        def centre(k):
+            n = k // UNITS
+            neg_mean = tiles["neg_mean", k]
+            sq_sum = stat.tile([P, UNIT_TILES], F32, tag="sq_sum")
+            yv = gate.tile([P, UNIT_TILES, D], F32, tag="yv")
+            for i in range(UNIT_TILES):
+                r = tiles["r%d" % i, k]
+                squares = norm.tile([P, D], BF16, tag="squares", bufs=4)
+                nc.scalar.activation(
+                    out=squares[:],
+                    in_=r[:],
+                    func=ACT.Square,
+                    bias=neg_mean[:, i : i + 1],
+                    scale=1.0,
+                    accum_out=sq_sum[:, i : i + 1],
+                )
+                nc.vector.scalar_tensor_tensor(
+                    out=yv[:, i, :], in0=r[:], scalar=neg_mean[:, i : i + 1], in1=tiles["gain_shift", n][:, 0, :],
+                    op0=ALU.add, op1=ALU.mult,
+                )
+            tiles["yv", k] = yv
+            var_eps = stat.tile([P, UNIT_TILES], F32, tag="var_eps")
+            nc.scalar.activation(out=var_eps[:], in_=sq_sum[:], func=ACT.Copy, bias=EPS, scale=1.0 / D)
+            rstd = stat.tile([P, UNIT_TILES], F32, tag="rstd")
+            nc.gpsimd.tensor_tensor(out=rstd[:], in0=var_eps[:], in1=neg_half[:], op=ALU.pow)
+            tiles["rstd", k] = rstd
+
+        def unit_acc(k):
+            first = (k % UNITS) * UNIT_TILES
+            return acc[:, first : first + UNIT_TILES, :]
+
+        def scale_shift(k):
+            n = k // UNITS
+            yv = tiles["yv", k]
+            for i in range(UNIT_TILES):
+                nc.vector.scalar_tensor_tensor(
+                    out=yv[:, i, :],
+                    in0=yv[:, i, :],
+                    scalar=tiles["rstd", k][:, i : i + 1],
+                    in1=tiles["gain_shift", n][:, 1, :],
+                    op0=ALU.mult,
+                    op1=ALU.add,
+                )
+
+        def weigh(k):
+            yv = tiles["yv", k]
+            if k // UNITS == 0:
+                for i in range(UNIT_TILES):
+                    nc.gpsimd.tensor_tensor(
+                        out=unit_acc(k)[:, i, :], in0=yv[:, i, :], in1=tiles["sel_u", k][:, i, :], op=ALU.mult
+                    )
+            else:
+                nc.vector.tensor_tensor(out=yv[:], in0=yv[:], in1=tiles["sel_u", k][:], op=ALU.mult)
+
+        def accumulate(k, first_tile):
+            adder = nc.vector if k == TOTAL - 1 else nc.gpsimd
+            for i in range(first_tile, first_tile + UNIT_TILES // 2):
+                tile_no = (k % UNITS) * UNIT_TILES + i
+                if k // UNITS > 0:
+                    adder.tensor_tensor(
+                        out=acc[:, tile_no, :], in0=acc[:, tile_no, :], in1=tiles["yv", k][:, i, :], op=ALU.add
+                    )
+                if k // UNITS == VARS - 1:
+                    nc.sync.dma_start(out=out[tile_no * P : (tile_no + 1) * P, :], in_=acc[:, tile_no, :])
+
+        for step in range(-4, TOTAL + 1):
+            if live(step + 4):
+                load_hv(step + 4)
+            if live(step + 1):
+                load_x_sel(step + 1)
+            for m in (2 * step + 7, 2 * step + 8):
+                if live(m):
+                    weight_load(m)
+
+            for m in (2 * step + 3, 2 * step + 4):
+                if live(m):
+                    weight_quantise(m)
+            if live(step):
+                gate_layers(step)
+            if live(step + 1):
+                first_layer(step + 1)
+            if live(step):
+                residual(step)
+            if live(step + 2):
+                hv_transpose(step + 2, 0)
+            if live(step):
+                mean(step)
+            if live(step + 2):
+                hv_transpose(step + 2, 1)
+            if live(step - 1):
+                scale_shift(step - 1)
+            if live(step) and step % UNITS == 0:
+                spread_gain_shift(step // UNITS)
+            if live(step + 1):
+                e1_regroup(step + 1)
+            if live(step - 1):
+                weigh(step - 1)
+            if live(step + 1):
+                e1_quantise(step + 1)
+            if live(step - 1):
+                accumulate(step - 1, 0)
+            if live(step):
+                centre(step)
+            if live(step - 1):
+                accumulate(step - 1, UNIT_TILES // 2)
+            if live(step + 2):
+                hv_quantise(step + 2)
+            for m in (2 * step + 5, 2 * step + 6):
+                if live(m):
+                    weight_regroup(m)

@@ -40,7 +40,7 @@ def tile_variableselectionnetwork_pb_t_kernel(
         gate = ctx.enter_context(tc.tile_pool(name="gate", bufs=2))
         norm = ctx.enter_context(tc.tile_pool(name="norm", bufs=2 * UNIT_TILES))
         stat = ctx.enter_context(tc.tile_pool(name="stat", bufs=3))
-        psum = ctx.enter_context(tc.psum_pool(name="psum", bufs=4))
+        psum = ctx.enter_context(tc.psum_pool(name="psum", bufs=3))
 
         ident_f = const.tile([P, P], F32)
         make_identity(nc, ident_f[:])
@@ -90,19 +90,18 @@ def tile_variableselectionnetwork_pb_t_kernel(
             grouped = wstage.tile([P, D, PACK], BF16, tag="w_grp", align_bytes=64)
             tiles["w_grp", m] = grouped
             if m % 3 == 0:
-                permuted = grouped[:].rearrange("p (t m) j -> p t m j", t=PACK)
-                by_chunk = raw[:].rearrange("p j (m t) -> p t m j", t=PACK)
-                nc.vector.tensor_copy(out=permuted[:, 0:2], in_=by_chunk[:, 0:2])
-                nc.scalar.copy(out=permuted[:, 2:4], in_=by_chunk[:, 2:4])
-                return
-            nc.vector.tensor_copy(
-                out=grouped[:, 0:320, :].rearrange("p (c i) t -> p c t i", i=4),
-                in_=raw[:, :, 0:320].rearrange("p t (c i) -> p c t i", i=4),
-            )
-            nc.scalar.copy(
-                out=grouped[:, 320:D, :].rearrange("p (c i) t -> p c t i", i=4),
-                in_=raw[:, :, 320:D].rearrange("p t (c i) -> p c t i", i=4),
-            )
+                to = grouped[:].rearrange("p (t m) j -> p t m j", t=PACK)
+                fro = raw[:].rearrange("p j (m t) -> p t m j", t=PACK)
+                split = PACK // 2
+            else:
+                to = grouped[:].rearrange("p (c i) j -> p c j i", i=4)
+                fro = raw[:].rearrange("p j (c i) -> p c j i", i=4)
+                split = D // 4 // 2
+            if m < 3:
+                nc.vector.tensor_copy(out=to[:, :split], in_=fro[:, :split])
+                nc.scalar.copy(out=to[:, split:], in_=fro[:, split:])
+            else:
+                nc.scalar.copy(out=to, in_=fro)
 
         def weight_quantise(m):
             codes = wquant.tile([P, D], U32, tag="w_codes%d" % (m % 3), align_bytes=64)
@@ -115,14 +114,14 @@ def tile_variableselectionnetwork_pb_t_kernel(
             tiles["w_codes", m] = codes
             tiles["w_scales", m] = scales
 
-        def mx_pass(out_ps, m, c, codes, scales):
+        def mx_pass(out_ps, m, c, codes, scales, rows=slice(0, UNIT_ROWS)):
             feats = slice(c * P, (c + 1) * P)
             nc.tensor.matmul_mx(
                 out=out_ps,
                 lhsT=tiles["w_codes", m][:, feats].bitcast(FP8X4),
                 lhsT_scale=tiles["w_scales", m][:, feats],
-                rhs=codes[:].bitcast(FP8X4),
-                rhs_scale=scales[:],
+                rhs=codes[:, rows].bitcast(FP8X4),
+                rhs_scale=scales[:, rows],
                 start=True,
                 stop=True,
             )
@@ -176,21 +175,18 @@ def tile_variableselectionnetwork_pb_t_kernel(
 
         def first_layer(k):
             n = k // UNITS
-            planes = quant.tile([P, CHUNKS, UNIT_ROWS], BF16, tag="e1_planes")
-            for c in range(CHUNKS):
-                e1_ps = psum.tile([P, UNIT_ROWS], F32, tag="to_scalar")
-                mx_pass(e1_ps[:], 3 * n, c, tiles["hv_codes", k], tiles["hv_scales", k])
-                nc.scalar.activation(
-                    out=planes[:, c, :], in_=e1_ps[:], func=ACT.Identity, bias=vb1_cols[:, n, c : c + 1], scale=1.0
-                )
-            tiles["e1_planes", k] = planes
-
-        def e1_regroup(k):
             grouped = quant.tile([P, UNIT_ROWS, PACK], BF16, tag="e1_grp", align_bytes=64)
-            nc.vector.tensor_copy(
-                out=grouped[:].rearrange("p (b i) t -> p b t i", i=4),
-                in_=tiles["e1_planes", k][:].rearrange("p t (b i) -> p b t i", i=4),
-            )
+            for i in range(UNIT_TILES):
+                rows = slice(i * P, (i + 1) * P)
+                e1_ps = psum.tile([P, CHUNKS, P], F32, tag="to_vector", bufs=4)
+                for c in range(CHUNKS):
+                    mx_pass(e1_ps[:, c, :], 3 * n, c, tiles["hv_codes", k], tiles["hv_scales", k], rows)
+                nc.vector.tensor_tensor(
+                    out=grouped[:, rows, :],
+                    in0=e1_ps[:].rearrange("p c b -> p b c"),
+                    in1=vb1_cols[:, n, :].unsqueeze(1).to_broadcast([P, P, CHUNKS]),
+                    op=ALU.add,
+                )
             tiles["e1_grp", k] = grouped
 
         def e1_quantise(k):
@@ -210,7 +206,7 @@ def tile_variableselectionnetwork_pb_t_kernel(
             for c in range(CHUNKS):
                 g4_ps = psum.tile([P, UNIT_ROWS], F32, tag="to_scalar")
                 mx_pass(g4_ps[:], 3 * n + 1, c, tiles["e1_codes", k], tiles["e1_scales", k])
-                g5_ps = psum.tile([P, UNIT_ROWS], F32, tag="to_vector", bufs=3)
+                g5_ps = psum.tile([P, UNIT_ROWS], F32, tag="to_vector", bufs=4)
                 mx_pass(g5_ps[:], 3 * n + 2, c, tiles["e1_codes", k], tiles["e1_scales", k])
                 sig = gate.tile([P, UNIT_ROWS], F32, tag="sig", bufs=3)
                 nc.scalar.activation(
@@ -263,36 +259,39 @@ def tile_variableselectionnetwork_pb_t_kernel(
                 )
             tiles["gain_shift", n] = gs_ps
 
-        def centre(k):
-            n = k // UNITS
-            neg_mean = tiles["neg_mean", k]
+        def squares(k):
             sq_sum = stat.tile([P, UNIT_TILES], F32, tag="sq_sum")
-            yv = gate.tile([P, UNIT_TILES, D], F32, tag="yv")
             for i in range(UNIT_TILES):
-                r = tiles["r%d" % i, k]
-                squares = norm.tile([P, D], BF16, tag="squares", bufs=4)
+                sq = norm.tile([P, D], BF16, tag="squares", bufs=4)
                 nc.scalar.activation(
-                    out=squares[:],
-                    in_=r[:],
+                    out=sq[:],
+                    in_=tiles["r%d" % i, k][:],
                     func=ACT.Square,
-                    bias=neg_mean[:, i : i + 1],
+                    bias=tiles["neg_mean", k][:, i : i + 1],
                     scale=1.0,
                     accum_out=sq_sum[:, i : i + 1],
                 )
-                nc.vector.scalar_tensor_tensor(
-                    out=yv[:, i, :], in0=r[:], scalar=neg_mean[:, i : i + 1], in1=tiles["gain_shift", n][:, 0, :],
-                    op0=ALU.add, op1=ALU.mult,
-                )
-            tiles["yv", k] = yv
             var_eps = stat.tile([P, UNIT_TILES], F32, tag="var_eps")
             nc.scalar.activation(out=var_eps[:], in_=sq_sum[:], func=ACT.Copy, bias=EPS, scale=1.0 / D)
-            rstd = stat.tile([P, UNIT_TILES], F32, tag="rstd")
-            nc.gpsimd.tensor_tensor(out=rstd[:], in0=var_eps[:], in1=neg_half[:], op=ALU.pow)
-            tiles["rstd", k] = rstd
+            tiles["var_eps", k] = var_eps
 
-        def unit_acc(k):
-            first = (k % UNITS) * UNIT_TILES
-            return acc[:, first : first + UNIT_TILES, :]
+        def centre(k):
+            yv = gate.tile([P, UNIT_TILES, D], F32, tag="yv", bufs=3)
+            for i in range(UNIT_TILES):
+                nc.vector.scalar_tensor_tensor(
+                    out=yv[:, i, :],
+                    in0=tiles["r%d" % i, k][:],
+                    scalar=tiles["neg_mean", k][:, i : i + 1],
+                    in1=tiles["gain_shift", k // UNITS][:, 0, :],
+                    op0=ALU.add,
+                    op1=ALU.mult,
+                )
+            tiles["yv", k] = yv
+
+        def inverse_std(k):
+            rstd = stat.tile([P, UNIT_TILES], F32, tag="rstd")
+            nc.gpsimd.tensor_tensor(out=rstd[:], in0=tiles["var_eps", k][:], in1=neg_half[:], op=ALU.pow)
+            tiles["rstd", k] = rstd
 
         def scale_shift(k):
             n = k // UNITS
@@ -307,69 +306,63 @@ def tile_variableselectionnetwork_pb_t_kernel(
                     op1=ALU.add,
                 )
 
-        def weigh(k):
-            yv = tiles["yv", k]
+        def weigh(k, i):
+            engine = nc.vector if (k == TOTAL - 1 and i > 0) or (k == TOTAL - 2 and i > 1) else nc.gpsimd
+            tile_no = (k % UNITS) * UNIT_TILES + i
+            total = acc[:, tile_no, :]
+            y = tiles["yv", k][:, i, :]
+            weights = tiles["sel_u", k][:, i, :]
             if k // UNITS == 0:
-                for i in range(UNIT_TILES):
-                    nc.gpsimd.tensor_tensor(
-                        out=unit_acc(k)[:, i, :], in0=yv[:, i, :], in1=tiles["sel_u", k][:, i, :], op=ALU.mult
-                    )
-            else:
-                nc.vector.tensor_tensor(out=yv[:], in0=yv[:], in1=tiles["sel_u", k][:], op=ALU.mult)
+                engine.tensor_tensor(out=total, in0=y, in1=weights, op=ALU.mult)
+                return
+            engine.tensor_tensor(out=y, in0=y, in1=weights, op=ALU.mult)
+            engine.tensor_tensor(out=total, in0=total, in1=y, op=ALU.add)
+            if k // UNITS == VARS - 1:
+                nc.sync.dma_start(out=out[tile_no * P : (tile_no + 1) * P, :], in_=total)
 
-        def accumulate(k, first_tile):
-            adder = nc.vector if k == TOTAL - 1 else nc.gpsimd
-            for i in range(first_tile, first_tile + UNIT_TILES // 2):
-                tile_no = (k % UNITS) * UNIT_TILES + i
-                if k // UNITS > 0:
-                    adder.tensor_tensor(
-                        out=acc[:, tile_no, :], in0=acc[:, tile_no, :], in1=tiles["yv", k][:, i, :], op=ALU.add
-                    )
-                if k // UNITS == VARS - 1:
-                    nc.sync.dma_start(out=out[tile_no * P : (tile_no + 1) * P, :], in_=acc[:, tile_no, :])
+        def weights_at(step, lag, first):
+            return [m for m in range(3 * VARS) if step == (first + (m > 0) if m < 3 else m - lag)]
 
         for step in range(-4, TOTAL + 1):
             if live(step + 4):
                 load_hv(step + 4)
             if live(step + 1):
                 load_x_sel(step + 1)
-            for m in (2 * step + 7, 2 * step + 8):
-                if live(m):
-                    weight_load(m)
+            for m in weights_at(step, 6, -4):
+                weight_load(m)
 
-            for m in (2 * step + 3, 2 * step + 4):
-                if live(m):
+            if step < 0:
+                for m in weights_at(step, 3, -2):
                     weight_quantise(m)
             if live(step):
                 gate_layers(step)
+            if live(step + 2):
+                hv_transpose(step + 2, 0)
+                hv_transpose(step + 2, 1)
             if live(step + 1):
                 first_layer(step + 1)
             if live(step):
                 residual(step)
-            if live(step + 2):
-                hv_transpose(step + 2, 0)
-            if live(step):
                 mean(step)
             if live(step + 2):
-                hv_transpose(step + 2, 1)
+                hv_quantise(step + 2)
+            if step >= 0:
+                for m in weights_at(step, 3, -2):
+                    weight_quantise(m)
+            if live(step + 1):
+                e1_quantise(step + 1)
             if live(step - 1):
                 scale_shift(step - 1)
             if live(step) and step % UNITS == 0:
                 spread_gain_shift(step // UNITS)
-            if live(step + 1):
-                e1_regroup(step + 1)
             if live(step - 1):
-                weigh(step - 1)
-            if live(step + 1):
-                e1_quantise(step + 1)
-            if live(step - 1):
-                accumulate(step - 1, 0)
+                for i in range(UNIT_TILES - 1):
+                    weigh(step - 1, i)
+            for m in weights_at(step, 4, -3):
+                weight_regroup(m)
             if live(step):
+                squares(step)
                 centre(step)
+                inverse_std(step)
             if live(step - 1):
-                accumulate(step - 1, UNIT_TILES // 2)
-            if live(step + 2):
-                hv_quantise(step + 2)
-            for m in (2 * step + 5, 2 * step + 6):
-                if live(m):
-                    weight_regroup(m)
+                weigh(step - 1, UNIT_TILES - 1)

@@ -22,6 +22,9 @@ UNIT_TILES = UNIT_ROWS // P
 UNITS = BATCH // UNIT_ROWS
 TOTAL = VARS * UNITS
 EPS = 1e-5
+EARLY = 3
+SCALAR_BANKS, VECTOR_BANKS, SEL_BANKS = 3, 3, 2
+TAIL = TOTAL - 3
 
 FLOPS = 3 * VARS * 2 * BATCH * D * D
 
@@ -34,13 +37,13 @@ def tile_variableselectionnetwork_pb_t_kernel(
         ctx.enter_context(tc.manual_schedule())
         const = ctx.enter_context(tc.tile_pool(name="const", bufs=1))
         wstage = ctx.enter_context(tc.tile_pool(name="wstage", bufs=2))
-        wquant = ctx.enter_context(tc.tile_pool(name="wquant", bufs=VARS))
+        wquant = ctx.enter_context(tc.tile_pool(name="wquant", bufs=2))
         loads = ctx.enter_context(tc.tile_pool(name="loads", bufs=4))
         quant = ctx.enter_context(tc.tile_pool(name="quant", bufs=2))
         gate = ctx.enter_context(tc.tile_pool(name="gate", bufs=2))
         norm = ctx.enter_context(tc.tile_pool(name="norm", bufs=2 * UNIT_TILES))
         stat = ctx.enter_context(tc.tile_pool(name="stat", bufs=3))
-        psum = ctx.enter_context(tc.psum_pool(name="psum", bufs=3))
+        psum = ctx.enter_context(tc.psum_pool(name="psum", bufs=SCALAR_BANKS))
 
         ident_f = const.tile([P, P], F32)
         make_identity(nc, ident_f[:])
@@ -63,15 +66,10 @@ def tile_variableselectionnetwork_pb_t_kernel(
         nc.scalar.dma_start(out=gs_rows[0:VARS, :], in_=vlng)
         nc.scalar.dma_start(out=gs_rows[VARS : 2 * VARS, :], in_=vlnb)
 
-        bias_ps = psum.tile([P, P], BF16, tag="to_scalar")
-        nc.tensor.transpose(bias_ps[:], bias_rows[:], ident_b[:])
+        acc = const.tile([P, UNITS, CHUNKS, UNIT_ROWS], F32)
+
         bias_cols = const.tile([P, 2, VARS, CHUNKS], F32)
-        nc.scalar.copy(
-            out=bias_cols[:].rearrange("p k n c -> p (k n c)"), in_=bias_ps[:, 0 : 2 * VARS * CHUNKS]
-        )
-
-
-        acc = const.tile([P, BATCH // P, D], F32)
+        gs_cols = const.tile([P, 2 * VARS, 2, 2], F32)
 
         tiles = {}
 
@@ -80,7 +78,7 @@ def tile_variableselectionnetwork_pb_t_kernel(
 
         def weight_load(m):
             n = m // 3
-            raw = wstage.tile([P, PACK, D], BF16, tag="w_raw", bufs=4)
+            raw = wstage.tile([P, PACK, D], BF16, tag="w_raw", bufs=5)
             w = (vW1, vW4, vW5)[m % 3]
             nc.sync.dma_start(out=raw[:], in_=w[n].rearrange("(p t) c -> p t c", t=PACK))
             tiles["w_raw", m] = raw
@@ -97,11 +95,11 @@ def tile_variableselectionnetwork_pb_t_kernel(
                 to = grouped[:].rearrange("p (c i) j -> p c j i", i=4)
                 fro = raw[:].rearrange("p j (c i) -> p c j i", i=4)
                 split = D // 4 // 2
-            if m < 3:
+            if m < 99:
                 nc.vector.tensor_copy(out=to[:, :split], in_=fro[:, :split])
                 nc.scalar.copy(out=to[:, split:], in_=fro[:, split:])
             else:
-                nc.scalar.copy(out=to, in_=fro)
+                nc.vector.tensor_copy(out=to, in_=fro)
 
         def weight_quantise(m):
             codes = wquant.tile([P, D], U32, tag="w_codes%d" % (m % 3), align_bytes=64)
@@ -126,21 +124,40 @@ def tile_variableselectionnetwork_pb_t_kernel(
                 stop=True,
             )
 
+        def column_constants():
+            bias_ps = psum.tile([P, P], BF16, tag="to_scalar")
+            nc.tensor.transpose(bias_ps[:], bias_rows[:], ident_b[:])
+            nc.scalar.copy(
+                out=bias_cols[:].rearrange("p k n c -> p (k n c)"), in_=bias_ps[:, 0 : 2 * VARS * CHUNKS]
+            )
+            gs_ps = psum.tile([P, 2, P], F32, tag="to_scalar")
+            gs_words = gs_rows[:].bitcast(F32)
+            for u in range(2):
+                nc.tensor.transpose(gs_ps[:, u, :], gs_words[:, u * P : (u + 1) * P], ident_f[:])
+            nc.scalar.copy(
+                out=gs_cols[:],
+                in_=gs_ps[:].rearrange("p u r -> p (u r)").bitcast(BF16).rearrange("p (u r e) -> p r u e", u=2, e=2)[
+                    :, 0 : 2 * VARS
+                ],
+            )
+
         def unit_rows(dram, k):
             first = (k % UNITS) * UNIT_ROWS
             return dram[first : first + UNIT_ROWS, k // UNITS, :].rearrange("(i p) d -> p i d", p=P)
 
         def load_hv(k):
-            hv_u = loads.tile([P, UNIT_TILES * D], BF16, tag="hv_u")
+            hv_u = loads.tile([P, UNIT_TILES * D], BF16, tag="hv_u", bufs=3)
             nc.sync.dma_start(out=hv_u[:].rearrange("p (i d) -> p i d", i=UNIT_TILES), in_=unit_rows(hv, k))
             tiles["hv_u", k] = hv_u
 
-        def load_x_sel(k):
+        def load_x(k):
             x_u = loads.tile([P, UNIT_TILES, D], BF16, tag="x_u", bufs=3)
             nc.sync.dma_start(out=x_u[:], in_=unit_rows(x, k))
-            sel_u = loads.tile([P, UNIT_TILES, D], BF16, tag="sel_u")
-            nc.sync.dma_start(out=sel_u[:], in_=unit_rows(sel_w, k))
             tiles["x_u", k] = x_u
+
+        def load_sel(k):
+            sel_u = loads.tile([P, UNIT_TILES, D], BF16, tag="sel_u", bufs=3)
+            nc.sync.dma_start(out=sel_u[:], in_=unit_rows(sel_w, k))
             tiles["sel_u", k] = sel_u
 
         def hv_transpose(k, half):
@@ -151,7 +168,13 @@ def tile_variableselectionnetwork_pb_t_kernel(
                 hv_grp = tiles["hv_grp", k]
             hv_grp_words = hv_grp[:].bitcast(F32).rearrange("p (b u) -> p b u", u=2)
             if True:
-                hv_t = psum.tile([P, 2, 2 * P], F32, tag="to_scalar")
+                on_scalar = k < EARLY
+                hv_t = psum.tile(
+                    [P, 2, 2 * P],
+                    F32,
+                    tag="to_scalar" if on_scalar else "to_vector",
+                    bufs=SCALAR_BANKS if on_scalar else VECTOR_BANKS,
+                )
                 for u in range(2):
                     for j in range(2):
                         i = 2 * half + j
@@ -160,10 +183,11 @@ def tile_variableselectionnetwork_pb_t_kernel(
                             hv_words[:, i * 2 * P + u : (i + 1) * 2 * P : 2],
                             ident_f[:],
                         )
-                nc.scalar.copy(
-                    out=hv_grp_words[:, half * 2 * P : (half + 1) * 2 * P, :],
-                    in_=hv_t[:].rearrange("p u b -> p b u"),
-                )
+                to = hv_grp_words[:, half * 2 * P : (half + 1) * 2 * P, :]
+                if on_scalar:
+                    nc.scalar.copy(out=to, in_=hv_t[:].rearrange("p u b -> p b u"))
+                else:
+                    nc.vector.tensor_copy(out=to, in_=hv_t[:].rearrange("p u b -> p b u"))
             tiles["hv_grp", k] = hv_grp
 
         def hv_quantise(k):
@@ -173,21 +197,22 @@ def tile_variableselectionnetwork_pb_t_kernel(
             tiles["hv_codes", k] = codes
             tiles["hv_scales", k] = scales
 
-        def first_layer(k):
+        def first_layer(k, i):
             n = k // UNITS
-            grouped = quant.tile([P, UNIT_ROWS, PACK], BF16, tag="e1_grp", align_bytes=64)
-            for i in range(UNIT_TILES):
-                rows = slice(i * P, (i + 1) * P)
-                e1_ps = psum.tile([P, CHUNKS, P], F32, tag="to_vector", bufs=4)
-                for c in range(CHUNKS):
-                    mx_pass(e1_ps[:, c, :], 3 * n, c, tiles["hv_codes", k], tiles["hv_scales", k], rows)
-                nc.vector.tensor_tensor(
-                    out=grouped[:, rows, :],
-                    in0=e1_ps[:].rearrange("p c b -> p b c"),
-                    in1=vb1_cols[:, n, :].unsqueeze(1).to_broadcast([P, P, CHUNKS]),
-                    op=ALU.add,
-                )
-            tiles["e1_grp", k] = grouped
+            if i == 0:
+                grouped = quant.tile([P, UNIT_ROWS, PACK], BF16, tag="e1_grp", align_bytes=64)
+                tiles["e1_grp", k] = grouped
+            grouped = tiles["e1_grp", k]
+            rows = slice(i * P, (i + 1) * P)
+            e1_ps = psum.tile([P, CHUNKS, P], F32, tag="to_vector", bufs=VECTOR_BANKS)
+            for c in range(CHUNKS):
+                mx_pass(e1_ps[:, c, :], 3 * n, c, tiles["hv_codes", k], tiles["hv_scales", k], rows)
+            nc.vector.tensor_tensor(
+                out=grouped[:, rows, :],
+                in0=e1_ps[:].rearrange("p c b -> p b c"),
+                in1=vb1_cols[:, n, :].unsqueeze(1).to_broadcast([P, P, CHUNKS]),
+                op=ALU.add,
+            )
 
         def e1_quantise(k):
             codes = quant.tile([P, UNIT_ROWS], U32, tag="e1_codes", align_bytes=64)
@@ -202,11 +227,11 @@ def tile_variableselectionnetwork_pb_t_kernel(
 
         def gate_layers(k):
             n = k // UNITS
-            gv_t = gate.tile([P, CHUNKS, UNIT_ROWS], F32, tag="gv_t")
+            gv_t = gate.tile([P, CHUNKS, UNIT_ROWS], F32, tag="gv_t", bufs=1)
             for c in range(CHUNKS):
                 g4_ps = psum.tile([P, UNIT_ROWS], F32, tag="to_scalar")
                 mx_pass(g4_ps[:], 3 * n + 1, c, tiles["e1_codes", k], tiles["e1_scales", k])
-                g5_ps = psum.tile([P, UNIT_ROWS], F32, tag="to_vector", bufs=4)
+                g5_ps = psum.tile([P, UNIT_ROWS], F32, tag="to_vector", bufs=VECTOR_BANKS)
                 mx_pass(g5_ps[:], 3 * n + 2, c, tiles["e1_codes", k], tiles["e1_scales", k])
                 sig = gate.tile([P, UNIT_ROWS], F32, tag="sig", bufs=3)
                 nc.scalar.activation(
@@ -222,42 +247,52 @@ def tile_variableselectionnetwork_pb_t_kernel(
                 )
             tiles["gv_t", k] = gv_t
 
-        def residual(k):
-            row_sum = stat.tile([P, UNIT_TILES], F32, tag="row_sum")
-            for i in range(UNIT_TILES):
-                r_ps = psum.tile([P, D], F32, tag="to_scalar")
-                nc.tensor.matmul(out=r_ps[:], lhsT=ident_b[:], rhs=tiles["x_u", k][:, i, :], start=True, stop=False)
-                for c in range(CHUNKS):
-                    nc.tensor.matmul(
-                        out=r_ps[:, c * P : (c + 1) * P],
-                        lhsT=tiles["gv_t", k][:, c, i * P : (i + 1) * P],
-                        rhs=ident_f[:],
-                        is_transpose=True,
-                        start=False,
-                        stop=(c == CHUNKS - 1),
-                    )
-                r = norm.tile([P, D], F32, tag="r")
-                nc.scalar.activation(out=r[:], in_=r_ps[:], func=ACT.Identity, accum_out=row_sum[:, i : i + 1])
-                tiles["r%d" % i, k] = r
-            tiles["row_sum", k] = row_sum
+        def residual(k, i):
+            if i == 0 and k == TOTAL - 1:
+                mean_var = stat.tile([P, UNIT_TILES, 2], F32, tag="mean_var")
+                tiles["mean_var", k] = mean_var
+            elif i == 0:
+                row_sum = stat.tile([P, UNIT_TILES], F32, tag="row_sum")
+                tiles["row_sum", k] = row_sum
+            r_ps = psum.tile([P, D], F32, tag="to_scalar")
+            nc.tensor.matmul(out=r_ps[:], lhsT=ident_b[:], rhs=tiles["x_u", k][:, i, :], start=True, stop=False)
+            for c in range(CHUNKS):
+                nc.tensor.matmul(
+                    out=r_ps[:, c * P : (c + 1) * P],
+                    lhsT=tiles["gv_t", k][:, c, i * P : (i + 1) * P],
+                    rhs=ident_f[:],
+                    is_transpose=True,
+                    start=False,
+                    stop=(c == CHUNKS - 1),
+                )
+            r = norm.tile([P, D], F32, tag="r")
+            to = r[:].rearrange("p (u e w) -> p u e w", u=2, e=2)
+            fro = r_ps[:].rearrange("p (u w e) -> p u e w", u=2, e=2)
+            if k == TOTAL - 1:
+                nc.scalar.copy(out=to, in_=fro)
+                moments = stat.tile([P, 6], F32, tag="moments")
+                nc.vector.bn_stats(out=moments[:], in_=r[:])
+                nc.vector.bn_aggr(out=tiles["mean_var", k][:, i, :], in_=moments[:])
+            else:
+                nc.scalar.activation(out=to, in_=fro, func=ACT.Identity, accum_out=tiles["row_sum", k][:, i : i + 1])
+            tiles["r%d" % i, k] = r
+
+        def last_statistics(k):
+            neg_mean = stat.tile([P, UNIT_TILES], F32, tag="neg_mean")
+            nc.vector.tensor_scalar(
+                out=neg_mean[:], in0=tiles["mean_var", k][:, :, 0], scalar1=-1.0, scalar2=None, op0=ALU.mult
+            )
+            var_eps = stat.tile([P, UNIT_TILES], F32, tag="var_eps")
+            nc.vector.tensor_scalar(
+                out=var_eps[:], in0=tiles["mean_var", k][:, :, 1], scalar1=EPS, scalar2=None, op0=ALU.add
+            )
+            tiles["neg_mean", k] = neg_mean
+            tiles["var_eps", k] = var_eps
 
         def mean(k):
             neg_mean = stat.tile([P, UNIT_TILES], F32, tag="neg_mean")
             nc.scalar.mul(out=neg_mean[:], in_=tiles["row_sum", k][:], mul=-1.0 / D)
             tiles["neg_mean", k] = neg_mean
-
-        def spread_gain_shift(n):
-            gs_ps = psum.tile([P, 2, D], BF16, tag="gain_shift", bufs=1)
-            for v in range(2):
-                row = v * VARS + n
-                nc.tensor.matmul(
-                    out=gs_ps[:, v, :],
-                    lhsT=ident_b[:, row : row + 1].to_broadcast([P, P]),
-                    rhs=gs_rows[:],
-                    start=True,
-                    stop=True,
-                )
-            tiles["gain_shift", n] = gs_ps
 
         def squares(k):
             sq_sum = stat.tile([P, UNIT_TILES], F32, tag="sq_sum")
@@ -275,94 +310,157 @@ def tile_variableselectionnetwork_pb_t_kernel(
             nc.scalar.activation(out=var_eps[:], in_=sq_sum[:], func=ACT.Copy, bias=EPS, scale=1.0 / D)
             tiles["var_eps", k] = var_eps
 
-        def centre(k):
-            yv = gate.tile([P, UNIT_TILES, D], F32, tag="yv", bufs=3)
+        def normalise(k):
+            rstd = stat.tile([P, UNIT_TILES], F32, tag="rstd")
+            nc.gpsimd.tensor_tensor(out=rstd[:], in0=tiles["var_eps", k][:], in1=neg_half[:], op=ALU.pow)
+            z = gate.tile([P, UNIT_TILES, D], F32, tag="z", bufs=2)
             for i in range(UNIT_TILES):
-                nc.vector.scalar_tensor_tensor(
-                    out=yv[:, i, :],
+                engine = nc.vector if k == TOTAL - 1 and i % 2 == 1 else nc.gpsimd
+                engine.tensor_scalar(
+                    out=z[:, i, :],
                     in0=tiles["r%d" % i, k][:],
-                    scalar=tiles["neg_mean", k][:, i : i + 1],
-                    in1=tiles["gain_shift", k // UNITS][:, 0, :],
+                    scalar1=tiles["neg_mean", k][:, i : i + 1],
+                    scalar2=rstd[:, i : i + 1],
                     op0=ALU.add,
                     op1=ALU.mult,
                 )
-            tiles["yv", k] = yv
+            tiles["z", k] = z
 
-        def inverse_std(k):
-            rstd = stat.tile([P, UNIT_TILES], F32, tag="rstd")
-            nc.gpsimd.tensor_tensor(out=rstd[:], in0=tiles["var_eps", k][:], in1=neg_half[:], op=ALU.pow)
-            tiles["rstd", k] = rstd
+        def sel_transpose(k):
+            words = tiles["sel_u", k][:].rearrange("p i d -> p (i d)").bitcast(F32)
+            for u in range(2):
+                sel_ps = psum.tile([P, UNIT_ROWS], F32, tag="sel", bufs=SEL_BANKS)
+                for i in range(UNIT_TILES):
+                    first = (2 * i + u) * P
+                    nc.tensor.transpose(sel_ps[:, i * P : (i + 1) * P], words[:, first : first + P], ident_f[:])
+                tiles["sel_ps%d" % u, k] = sel_ps
 
-        def scale_shift(k):
+        def gain_shift(k, chunks):
             n = k // UNITS
-            yv = tiles["yv", k]
-            for i in range(UNIT_TILES):
-                nc.vector.scalar_tensor_tensor(
-                    out=yv[:, i, :],
-                    in0=yv[:, i, :],
-                    scalar=tiles["rstd", k][:, i : i + 1],
-                    in1=tiles["gain_shift", n][:, 1, :],
-                    op0=ALU.mult,
-                    op1=ALU.add,
+            for q in chunks:
+                u, e = divmod(q, 2)
+                z_ps = psum.tile([P, UNIT_ROWS], F32, tag="to_scalar")
+                for i in range(UNIT_TILES):
+                    nc.tensor.transpose(
+                        z_ps[:, i * P : (i + 1) * P], tiles["z", k][:, i, q * P : (q + 1) * P], ident_f[:]
+                    )
+                y = gate.tile([P, UNIT_ROWS], F32, tag="y", bufs=4)
+                gain = gs_cols[:, n, u, e : e + 1]
+                shift = gs_cols[:, VARS + n, u, e : e + 1]
+                if k >= TAIL and e == 1:
+                    nc.vector.tensor_scalar(
+                        out=y[:], in0=z_ps[:], scalar1=gain, scalar2=shift, op0=ALU.mult, op1=ALU.add
+                    )
+                else:
+                    nc.scalar.activation(out=y[:], in_=z_ps[:], func=ACT.Identity, bias=shift, scale=gain)
+                tiles["y%d" % q, k] = y
+
+        def weigh(k):
+            if k // UNITS == 0:
+                product = acc[:, k % UNITS, :, :]
+            else:
+                product_tile = gate.tile([P, CHUNKS, UNIT_ROWS], F32, tag="product", bufs=3)
+                product = product_tile[:]
+            for q in range(CHUNKS):
+                u, e = divmod(q, 2)
+                nc.vector.tensor_tensor(
+                    out=product[:, q, :],
+                    in0=tiles["y%d" % q, k][:],
+                    in1=tiles["sel_ps%d" % u, k][:].bitcast(BF16).rearrange("p (b e) -> p e b", e=2)[:, e, :],
+                    op=ALU.mult,
+                )
+            tiles["product", k] = product
+
+        def accumulate(k, chunks):
+            total = acc[:, k % UNITS, :, :]
+            for q in chunks:
+                nc.gpsimd.tensor_tensor(
+                    out=total[:, q, :], in0=total[:, q, :], in1=tiles["product", k][:, q, :], op=ALU.add
                 )
 
-        def weigh(k, i):
-            engine = nc.vector if (k == TOTAL - 1 and i > 0) or (k == TOTAL - 2 and i > 1) else nc.gpsimd
-            tile_no = (k % UNITS) * UNIT_TILES + i
-            total = acc[:, tile_no, :]
-            y = tiles["yv", k][:, i, :]
-            weights = tiles["sel_u", k][:, i, :]
-            if k // UNITS == 0:
-                engine.tensor_tensor(out=total, in0=y, in1=weights, op=ALU.mult)
-                return
-            engine.tensor_tensor(out=y, in0=y, in1=weights, op=ALU.mult)
-            engine.tensor_tensor(out=total, in0=total, in1=y, op=ALU.add)
-            if k // UNITS == VARS - 1:
-                nc.sync.dma_start(out=out[tile_no * P : (tile_no + 1) * P, :], in_=total)
+        def finish(k):
+            parts = [acc[:, k % UNITS, :, :], tiles["product", k]]
+            for i in range(UNIT_TILES):
+                rows = slice(i * P, (i + 1) * P)
+                out_ps = psum.tile([P, D], F32, tag="to_scalar")
+                for q in range(CHUNKS):
+                    for part, operand in enumerate(parts):
+                        nc.tensor.matmul(
+                            out=out_ps[:, q * P : (q + 1) * P],
+                            lhsT=operand[:, q, rows],
+                            rhs=ident_f[:],
+                            is_transpose=True,
+                            start=(part == 0),
+                            stop=(part == len(parts) - 1),
+                        )
+                result = norm.tile([P, D], F32, tag="result", bufs=UNIT_TILES)
+                to = result[:].rearrange("p (u w e) -> p u w e", u=2, e=2)
+                fro = out_ps[:].rearrange("p (u e w) -> p u w e", u=2, e=2)
+                if i % 2 == 0 or k < TOTAL - 1:
+                    nc.scalar.copy(out=to, in_=fro)
+                else:
+                    nc.vector.tensor_copy(out=to, in_=fro)
+                first = (k % UNITS) * UNIT_ROWS + i * P
+                nc.sync.dma_start(out=out[first : first + P, :], in_=result[:])
 
-        def weights_at(step, lag, first):
-            return [m for m in range(3 * VARS) if step == (first + (m > 0) if m < 3 else m - lag)]
+        def weights_at(late, early):
+            return [m for m in range(3 * VARS) if (step == early[m] if m < 3 else m == late)]
 
-        for step in range(-4, TOTAL + 1):
+        for step in range(-4, TOTAL + 3):
+            for m in weights_at(step + 6, (-4, -4, -4)):
+                if m != 1 and m != 2:
+                    weight_load(m)
             if live(step + 4):
                 load_hv(step + 4)
+            if step == -4:
+                weight_load(1)
+                weight_load(2)
             if live(step + 1):
-                load_x_sel(step + 1)
-            for m in weights_at(step, 6, -4):
-                weight_load(m)
+                load_x(step + 1)
+            if live(step):
+                load_sel(step)
 
-            if step < 0:
-                for m in weights_at(step, 3, -2):
-                    weight_quantise(m)
+            if step == TOTAL:
+                normalise(step - 1)
             if live(step):
                 gate_layers(step)
-            if live(step + 2):
-                hv_transpose(step + 2, 0)
-                hv_transpose(step + 2, 1)
+            if live(step - 2):
+                gain_shift(step - 2, (0, 1))
             if live(step + 1):
-                first_layer(step + 1)
-            if live(step):
-                residual(step)
-                mean(step)
-            if live(step + 2):
-                hv_quantise(step + 2)
-            if step >= 0:
-                for m in weights_at(step, 3, -2):
-                    weight_quantise(m)
+                first_layer(step + 1, 0)
+            if live(step - 2):
+                gain_shift(step - 2, (2, 3))
+            if live(step + 1):
+                for i in range(1, UNIT_TILES):
+                    first_layer(step + 1, i)
+            if live(step - 2):
+                sel_transpose(step - 2)
+            for m in weights_at(step + 4, (-4, -3, -3)):
+                weight_regroup(m)
             if live(step + 1):
                 e1_quantise(step + 1)
-            if live(step - 1):
-                scale_shift(step - 1)
-            if live(step) and step % UNITS == 0:
-                spread_gain_shift(step // UNITS)
-            if live(step - 1):
-                for i in range(UNIT_TILES - 1):
-                    weigh(step - 1, i)
-            for m in weights_at(step, 4, -3):
-                weight_regroup(m)
+            for m in weights_at(step + 3, (-4, -3, -3)):
+                weight_quantise(m)
+            if live(step + 2):
+                hv_quantise(step + 2)
+            if live(step - 1) and live(step):
+                squares(step - 1)
+                normalise(step - 1)
+            if live(step + 3):
+                hv_transpose(step + 3, 0)
+                hv_transpose(step + 3, 1)
+            if live(step - 2):
+                weigh(step - 2)
+            if live(step - 2) and 0 < (step - 2) // UNITS < VARS - 1:
+                accumulate(step - 2, range(CHUNKS))
             if live(step):
-                squares(step)
-                centre(step)
-                inverse_std(step)
-            if live(step - 1):
-                weigh(step - 1, UNIT_TILES - 1)
+                for i in range(UNIT_TILES):
+                    residual(step, i)
+                if step == TOTAL - 1:
+                    last_statistics(step)
+                else:
+                    mean(step)
+            if step == -3:
+                column_constants()
+            if live(step - 3) and (step - 3) // UNITS == VARS - 1:
+                finish(step - 3)

@@ -247,6 +247,11 @@ def tile_variableselectionnetwork_pb_t_kernel(
                 )
             tiles["gv_t", k] = gv_t
 
+        def open_residual(k, i):
+            r_ps = psum.tile([P, D], F32, tag="to_scalar")
+            nc.tensor.matmul(out=r_ps[:], lhsT=ident_b[:], rhs=tiles["x_u", k][:, i, :], start=True, stop=False)
+            tiles["r_ps%d" % i, k] = r_ps
+
         def residual(k, i):
             if i == 0 and k == TOTAL - 1:
                 mean_var = stat.tile([P, UNIT_TILES, 2], F32, tag="mean_var")
@@ -254,8 +259,7 @@ def tile_variableselectionnetwork_pb_t_kernel(
             elif i == 0:
                 row_sum = stat.tile([P, UNIT_TILES], F32, tag="row_sum")
                 tiles["row_sum", k] = row_sum
-            r_ps = psum.tile([P, D], F32, tag="to_scalar")
-            nc.tensor.matmul(out=r_ps[:], lhsT=ident_b[:], rhs=tiles["x_u", k][:, i, :], start=True, stop=False)
+            r_ps = tiles["r_ps%d" % i, k]
             for c in range(CHUNKS):
                 nc.tensor.matmul(
                     out=r_ps[:, c * P : (c + 1) * P],
@@ -315,7 +319,7 @@ def tile_variableselectionnetwork_pb_t_kernel(
             nc.gpsimd.tensor_tensor(out=rstd[:], in0=tiles["var_eps", k][:], in1=neg_half[:], op=ALU.pow)
             z = gate.tile([P, UNIT_TILES, D], F32, tag="z", bufs=2)
             for i in range(UNIT_TILES):
-                engine = nc.vector if k == TOTAL - 1 and i % 2 == 1 else nc.gpsimd
+                engine = nc.vector if k == TOTAL - 1 else nc.gpsimd
                 engine.tensor_scalar(
                     out=z[:, i, :],
                     in0=tiles["r%d" % i, k][:],
@@ -393,10 +397,10 @@ def tile_variableselectionnetwork_pb_t_kernel(
                             start=(part == 0),
                             stop=(part == len(parts) - 1),
                         )
-                result = norm.tile([P, D], F32, tag="result", bufs=UNIT_TILES)
+                result = norm.tile([P, D], F32, tag="result", bufs=2 * UNIT_TILES)
                 to = result[:].rearrange("p (u w e) -> p u w e", u=2, e=2)
                 fro = out_ps[:].rearrange("p (u e w) -> p u w e", u=2, e=2)
-                if i % 2 == 0 or k < TOTAL - 1:
+                if i % 2 == 0 or k < TOTAL - 2:
                     nc.scalar.copy(out=to, in_=fro)
                 else:
                     nc.vector.tensor_copy(out=to, in_=fro)
@@ -406,7 +410,7 @@ def tile_variableselectionnetwork_pb_t_kernel(
         def weights_at(late, early):
             return [m for m in range(3 * VARS) if (step == early[m] if m < 3 else m == late)]
 
-        for step in range(-4, TOTAL + 3):
+        for step in range(-4, TOTAL):
             for m in weights_at(step + 6, (-4, -4, -4)):
                 if m != 1 and m != 2:
                     weight_load(m)
@@ -420,8 +424,6 @@ def tile_variableselectionnetwork_pb_t_kernel(
             if live(step):
                 load_sel(step)
 
-            if step == TOTAL:
-                normalise(step - 1)
             if live(step):
                 gate_layers(step)
             if live(step - 2):
@@ -443,7 +445,7 @@ def tile_variableselectionnetwork_pb_t_kernel(
                 weight_quantise(m)
             if live(step + 2):
                 hv_quantise(step + 2)
-            if live(step - 1) and live(step):
+            if live(step - 1):
                 squares(step - 1)
                 normalise(step - 1)
             if live(step + 3):
@@ -454,13 +456,25 @@ def tile_variableselectionnetwork_pb_t_kernel(
             if live(step - 2) and 0 < (step - 2) // UNITS < VARS - 1:
                 accumulate(step - 2, range(CHUNKS))
             if live(step):
-                for i in range(UNIT_TILES):
+                for i in range(3):
+                    open_residual(step, i)
+                for i in range(UNIT_TILES - 1):
                     residual(step, i)
+                open_residual(step, UNIT_TILES - 1)
+                residual(step, UNIT_TILES - 1)
                 if step == TOTAL - 1:
                     last_statistics(step)
                 else:
                     mean(step)
             if step == -3:
                 column_constants()
-            if live(step - 3) and (step - 3) // UNITS == VARS - 1:
-                finish(step - 3)
+            if live(step - 2) and (step - 2) // UNITS == VARS - 1:
+                finish(step - 2)
+
+        normalise(TOTAL - 1)
+        for k in (TOTAL - 2, TOTAL - 1):
+            gain_shift(k, range(CHUNKS))
+            sel_transpose(k)
+            weigh(k)
+        for k in (TOTAL - 2, TOTAL - 1):
+            finish(k)

@@ -23,8 +23,7 @@ UNITS = BATCH // UNIT_ROWS
 TOTAL = VARS * UNITS
 EPS = 1e-5
 EARLY = 3
-SCALAR_BANKS, VECTOR_BANKS, SEL_BANKS = 3, 3, 2
-TAIL = TOTAL - 3
+SCALAR_BANKS, VECTOR_BANKS = 4, 4
 
 FLOPS = 3 * VARS * 2 * BATCH * D * D
 
@@ -66,10 +65,10 @@ def tile_variableselectionnetwork_pb_t_kernel(
         nc.scalar.dma_start(out=gs_rows[0:VARS, :], in_=vlng)
         nc.scalar.dma_start(out=gs_rows[VARS : 2 * VARS, :], in_=vlnb)
 
-        acc = const.tile([P, UNITS, CHUNKS, UNIT_ROWS], F32)
+        acc = const.tile([P, BATCH // P, D], F32)
 
         bias_cols = const.tile([P, 2, VARS, CHUNKS], F32)
-        gs_cols = const.tile([P, 2 * VARS, 2, 2], F32)
+        gs_cols = const.tile([P, CHUNKS, 2 * VARS], F32)
 
         tiles = {}
 
@@ -95,11 +94,8 @@ def tile_variableselectionnetwork_pb_t_kernel(
                 to = grouped[:].rearrange("p (c i) j -> p c j i", i=4)
                 fro = raw[:].rearrange("p j (c i) -> p c j i", i=4)
                 split = D // 4 // 2
-            if m < 99:
-                nc.vector.tensor_copy(out=to[:, :split], in_=fro[:, :split])
-                nc.scalar.copy(out=to[:, split:], in_=fro[:, split:])
-            else:
-                nc.vector.tensor_copy(out=to, in_=fro)
+            nc.vector.tensor_copy(out=to[:, :split], in_=fro[:, :split])
+            nc.scalar.copy(out=to[:, split:], in_=fro[:, split:])
 
         def weight_quantise(m):
             codes = wquant.tile([P, D], U32, tag="w_codes%d" % (m % 3), align_bytes=64)
@@ -130,16 +126,10 @@ def tile_variableselectionnetwork_pb_t_kernel(
             nc.scalar.copy(
                 out=bias_cols[:].rearrange("p k n c -> p (k n c)"), in_=bias_ps[:, 0 : 2 * VARS * CHUNKS]
             )
-            gs_ps = psum.tile([P, 2, P], F32, tag="to_scalar")
-            gs_words = gs_rows[:].bitcast(F32)
-            for u in range(2):
-                nc.tensor.transpose(gs_ps[:, u, :], gs_words[:, u * P : (u + 1) * P], ident_f[:])
-            nc.scalar.copy(
-                out=gs_cols[:],
-                in_=gs_ps[:].rearrange("p u r -> p (u r)").bitcast(BF16).rearrange("p (u r e) -> p r u e", u=2, e=2)[
-                    :, 0 : 2 * VARS
-                ],
-            )
+            gs_ps = psum.tile([P, CHUNKS, P], BF16, tag="to_scalar")
+            for c in range(CHUNKS):
+                nc.tensor.transpose(gs_ps[:, c, :], gs_rows[:, c * P : (c + 1) * P], ident_b[:])
+            nc.scalar.copy(out=gs_cols[:], in_=gs_ps[:, :, 0 : 2 * VARS])
 
         def unit_rows(dram, k):
             first = (k % UNITS) * UNIT_ROWS
@@ -247,11 +237,6 @@ def tile_variableselectionnetwork_pb_t_kernel(
                 )
             tiles["gv_t", k] = gv_t
 
-        def open_residual(k, i):
-            r_ps = psum.tile([P, D], F32, tag="to_scalar")
-            nc.tensor.matmul(out=r_ps[:], lhsT=ident_b[:], rhs=tiles["x_u", k][:, i, :], start=True, stop=False)
-            tiles["r_ps%d" % i, k] = r_ps
-
         def residual(k, i):
             if i == 0 and k == TOTAL - 1:
                 mean_var = stat.tile([P, UNIT_TILES, 2], F32, tag="mean_var")
@@ -259,7 +244,8 @@ def tile_variableselectionnetwork_pb_t_kernel(
             elif i == 0:
                 row_sum = stat.tile([P, UNIT_TILES], F32, tag="row_sum")
                 tiles["row_sum", k] = row_sum
-            r_ps = tiles["r_ps%d" % i, k]
+            r_ps = psum.tile([P, D], F32, tag="to_scalar")
+            nc.tensor.matmul(out=r_ps[:], lhsT=ident_b[:], rhs=tiles["x_u", k][:, i, :], start=True, stop=False)
             for c in range(CHUNKS):
                 nc.tensor.matmul(
                     out=r_ps[:, c * P : (c + 1) * P],
@@ -270,15 +256,15 @@ def tile_variableselectionnetwork_pb_t_kernel(
                     stop=(c == CHUNKS - 1),
                 )
             r = norm.tile([P, D], F32, tag="r")
-            to = r[:].rearrange("p (u e w) -> p u e w", u=2, e=2)
-            fro = r_ps[:].rearrange("p (u w e) -> p u e w", u=2, e=2)
             if k == TOTAL - 1:
-                nc.scalar.copy(out=to, in_=fro)
+                nc.scalar.copy(out=r[:], in_=r_ps[:])
                 moments = stat.tile([P, 6], F32, tag="moments")
                 nc.vector.bn_stats(out=moments[:], in_=r[:])
                 nc.vector.bn_aggr(out=tiles["mean_var", k][:, i, :], in_=moments[:])
             else:
-                nc.scalar.activation(out=to, in_=fro, func=ACT.Identity, accum_out=tiles["row_sum", k][:, i : i + 1])
+                nc.scalar.activation(
+                    out=r[:], in_=r_ps[:], func=ACT.Identity, accum_out=tiles["row_sum", k][:, i : i + 1]
+                )
             tiles["r%d" % i, k] = r
 
         def last_statistics(k):
@@ -330,82 +316,48 @@ def tile_variableselectionnetwork_pb_t_kernel(
                 )
             tiles["z", k] = z
 
-        def sel_transpose(k):
-            words = tiles["sel_u", k][:].rearrange("p i d -> p (i d)").bitcast(F32)
-            for u in range(2):
-                sel_ps = psum.tile([P, UNIT_ROWS], F32, tag="sel", bufs=SEL_BANKS)
-                for i in range(UNIT_TILES):
-                    first = (2 * i + u) * P
-                    nc.tensor.transpose(sel_ps[:, i * P : (i + 1) * P], words[:, first : first + P], ident_f[:])
-                tiles["sel_ps%d" % u, k] = sel_ps
-
         def gain_shift(k, chunks):
             n = k // UNITS
-            for q in chunks:
-                u, e = divmod(q, 2)
+            if 0 in chunks:
+                y = gate.tile([P, CHUNKS, UNIT_ROWS], F32, tag="y")
+                tiles["y", k] = y
+            y = tiles["y", k]
+            for c in chunks:
                 z_ps = psum.tile([P, UNIT_ROWS], F32, tag="to_scalar")
                 for i in range(UNIT_TILES):
                     nc.tensor.transpose(
-                        z_ps[:, i * P : (i + 1) * P], tiles["z", k][:, i, q * P : (q + 1) * P], ident_f[:]
+                        z_ps[:, i * P : (i + 1) * P], tiles["z", k][:, i, c * P : (c + 1) * P], ident_f[:]
                     )
-                y = gate.tile([P, UNIT_ROWS], F32, tag="y", bufs=4)
-                gain = gs_cols[:, n, u, e : e + 1]
-                shift = gs_cols[:, VARS + n, u, e : e + 1]
-                if k >= TAIL and e == 1:
+                gain = gs_cols[:, c, n : n + 1]
+                shift = gs_cols[:, c, VARS + n : VARS + n + 1]
+                if k in (TOTAL - 3, TOTAL - 1) and c % 2 == 1:
                     nc.vector.tensor_scalar(
-                        out=y[:], in0=z_ps[:], scalar1=gain, scalar2=shift, op0=ALU.mult, op1=ALU.add
+                        out=y[:, c, :], in0=z_ps[:], scalar1=gain, scalar2=shift, op0=ALU.mult, op1=ALU.add
                     )
                 else:
-                    nc.scalar.activation(out=y[:], in_=z_ps[:], func=ACT.Identity, bias=shift, scale=gain)
-                tiles["y%d" % q, k] = y
+                    nc.scalar.activation(out=y[:, c, :], in_=z_ps[:], func=ACT.Identity, bias=shift, scale=gain)
 
-        def weigh(k):
+        def weigh(k, i):
+            y_ps = psum.tile([P, D], F32, tag="to_vector", bufs=VECTOR_BANKS)
+            for c in range(CHUNKS):
+                nc.tensor.transpose(
+                    y_ps[:, c * P : (c + 1) * P], tiles["y", k][:, c, i * P : (i + 1) * P], ident_f[:]
+                )
             if k // UNITS == 0:
-                product = acc[:, k % UNITS, :, :]
+                product = acc[:, k % UNITS * UNIT_TILES + i, :]
             else:
-                product_tile = gate.tile([P, CHUNKS, UNIT_ROWS], F32, tag="product", bufs=3)
+                product_tile = norm.tile([P, D], F32, tag="product")
                 product = product_tile[:]
-            for q in range(CHUNKS):
-                u, e = divmod(q, 2)
-                nc.vector.tensor_tensor(
-                    out=product[:, q, :],
-                    in0=tiles["y%d" % q, k][:],
-                    in1=tiles["sel_ps%d" % u, k][:].bitcast(BF16).rearrange("p (b e) -> p e b", e=2)[:, e, :],
-                    op=ALU.mult,
-                )
-            tiles["product", k] = product
+            nc.vector.tensor_tensor(out=product, in0=y_ps[:], in1=tiles["sel_u", k][:, i, :], op=ALU.mult)
+            tiles["product%d" % i, k] = product
 
-        def accumulate(k, chunks):
-            total = acc[:, k % UNITS, :, :]
-            for q in chunks:
-                nc.gpsimd.tensor_tensor(
-                    out=total[:, q, :], in0=total[:, q, :], in1=tiles["product", k][:, q, :], op=ALU.add
-                )
-
-        def finish(k):
-            parts = [acc[:, k % UNITS, :, :], tiles["product", k]]
-            for i in range(UNIT_TILES):
-                rows = slice(i * P, (i + 1) * P)
-                out_ps = psum.tile([P, D], F32, tag="to_scalar")
-                for q in range(CHUNKS):
-                    for part, operand in enumerate(parts):
-                        nc.tensor.matmul(
-                            out=out_ps[:, q * P : (q + 1) * P],
-                            lhsT=operand[:, q, rows],
-                            rhs=ident_f[:],
-                            is_transpose=True,
-                            start=(part == 0),
-                            stop=(part == len(parts) - 1),
-                        )
-                result = norm.tile([P, D], F32, tag="result", bufs=2 * UNIT_TILES)
-                to = result[:].rearrange("p (u w e) -> p u w e", u=2, e=2)
-                fro = out_ps[:].rearrange("p (u e w) -> p u w e", u=2, e=2)
-                if i % 2 == 0 or k < TOTAL - 2:
-                    nc.scalar.copy(out=to, in_=fro)
-                else:
-                    nc.vector.tensor_copy(out=to, in_=fro)
-                first = (k % UNITS) * UNIT_ROWS + i * P
-                nc.sync.dma_start(out=out[first : first + P, :], in_=result[:])
+        def accumulate(k, i):
+            tile_no = k % UNITS * UNIT_TILES + i
+            total = acc[:, tile_no, :]
+            adder = nc.vector if k == TOTAL - 1 or (k == TOTAL - 2 and i > 0) else nc.gpsimd
+            adder.tensor_tensor(out=total, in0=total, in1=tiles["product%d" % i, k], op=ALU.add)
+            if k // UNITS == VARS - 1:
+                nc.sync.dma_start(out=out[tile_no * P : (tile_no + 1) * P, :], in_=total)
 
         def weights_at(late, early):
             return [m for m in range(3 * VARS) if (step == early[m] if m < 3 else m == late)]
@@ -435,8 +387,6 @@ def tile_variableselectionnetwork_pb_t_kernel(
             if live(step + 1):
                 for i in range(1, UNIT_TILES):
                     first_layer(step + 1, i)
-            if live(step - 2):
-                sel_transpose(step - 2)
             for m in weights_at(step + 4, (-4, -3, -3)):
                 weight_regroup(m)
             if live(step + 1):
@@ -448,33 +398,35 @@ def tile_variableselectionnetwork_pb_t_kernel(
             if live(step - 1):
                 squares(step - 1)
                 normalise(step - 1)
+            for i in range(UNIT_TILES):
+                if live(step - 2):
+                    weigh(step - 2, i)
+                if live(step):
+                    residual(step, i)
             if live(step + 3):
                 hv_transpose(step + 3, 0)
                 hv_transpose(step + 3, 1)
-            if live(step - 2):
-                weigh(step - 2)
-            if live(step - 2) and 0 < (step - 2) // UNITS < VARS - 1:
-                accumulate(step - 2, range(CHUNKS))
-            if live(step):
-                for i in range(3):
-                    open_residual(step, i)
-                for i in range(UNIT_TILES - 1):
-                    residual(step, i)
-                open_residual(step, UNIT_TILES - 1)
-                residual(step, UNIT_TILES - 1)
-                if step == TOTAL - 1:
-                    last_statistics(step)
-                else:
-                    mean(step)
+            if live(step) and step == TOTAL - 1:
+                last_statistics(step)
+            elif live(step):
+                mean(step)
+            if live(step - 2) and (step - 2) // UNITS > 0 and step < TOTAL - 1:
+                for i in range(UNIT_TILES):
+                    accumulate(step - 2, i)
             if step == -3:
                 column_constants()
-            if live(step - 2) and (step - 2) // UNITS == VARS - 1:
-                finish(step - 2)
 
         normalise(TOTAL - 1)
-        for k in (TOTAL - 2, TOTAL - 1):
-            gain_shift(k, range(CHUNKS))
-            sel_transpose(k)
-            weigh(k)
-        for k in (TOTAL - 2, TOTAL - 1):
-            finish(k)
+        gain_shift(TOTAL - 2, range(CHUNKS))
+        for i in range(UNIT_TILES):
+            weigh(TOTAL - 2, i)
+        gain_shift(TOTAL - 1, range(CHUNKS))
+        accumulate(TOTAL - 2, 0)
+        for i in range(UNIT_TILES):
+            accumulate(TOTAL - 3, i)
+        for i in range(UNIT_TILES):
+            weigh(TOTAL - 1, i)
+        for i in range(1, UNIT_TILES):
+            accumulate(TOTAL - 2, i)
+        for i in range(UNIT_TILES):
+            accumulate(TOTAL - 1, i)

@@ -23,6 +23,8 @@ UNITS = BATCH // UNIT_ROWS
 TOTAL = VARS * UNITS
 EPS = 1e-5
 EARLY = 3
+LAST = TOTAL - 1
+ADD_BY_VECTOR = [(k, i) for k in range(TOTAL - 3, TOTAL) for i in range(UNIT_TILES)]
 SCALAR_BANKS, VECTOR_BANKS = 4, 4
 
 FLOPS = 3 * VARS * 2 * BATCH * D * D
@@ -69,6 +71,7 @@ def tile_variableselectionnetwork_pb_t_kernel(
 
         bias_cols = const.tile([P, 2, VARS, CHUNKS], F32)
         gs_cols = const.tile([P, CHUNKS, 2 * VARS], F32)
+        gs_spread = const.tile([P, 2, D], BF16)
 
         tiles = {}
 
@@ -130,6 +133,17 @@ def tile_variableselectionnetwork_pb_t_kernel(
             for c in range(CHUNKS):
                 nc.tensor.transpose(gs_ps[:, c, :], gs_rows[:, c * P : (c + 1) * P], ident_b[:])
             nc.scalar.copy(out=gs_cols[:], in_=gs_ps[:, :, 0 : 2 * VARS])
+            spread_ps = psum.tile([P, 2, D], BF16, tag="to_scalar")
+            for v in range(2):
+                row = v * VARS + VARS - 1
+                nc.tensor.matmul(
+                    out=spread_ps[:, v, :],
+                    lhsT=ident_b[:, row : row + 1].to_broadcast([P, P]),
+                    rhs=gs_rows[:],
+                    start=True,
+                    stop=True,
+                )
+            nc.scalar.copy(out=gs_spread[:], in_=spread_ps[:])
 
         def unit_rows(dram, k):
             first = (k % UNITS) * UNIT_ROWS
@@ -158,7 +172,7 @@ def tile_variableselectionnetwork_pb_t_kernel(
                 hv_grp = tiles["hv_grp", k]
             hv_grp_words = hv_grp[:].bitcast(F32).rearrange("p (b u) -> p b u", u=2)
             if True:
-                on_scalar = k < EARLY
+                on_scalar = k < EARLY or (half == 1)
                 hv_t = psum.tile(
                     [P, 2, 2 * P],
                     F32,
@@ -244,7 +258,12 @@ def tile_variableselectionnetwork_pb_t_kernel(
             elif i == 0:
                 row_sum = stat.tile([P, UNIT_TILES], F32, tag="row_sum")
                 tiles["row_sum", k] = row_sum
-            r_ps = psum.tile([P, D], F32, tag="to_scalar")
+            r_ps = psum.tile(
+                [P, D],
+                F32,
+                tag="to_vector" if k == LAST else "to_scalar",
+                bufs=VECTOR_BANKS if k == LAST else SCALAR_BANKS,
+            )
             nc.tensor.matmul(out=r_ps[:], lhsT=ident_b[:], rhs=tiles["x_u", k][:, i, :], start=True, stop=False)
             for c in range(CHUNKS):
                 nc.tensor.matmul(
@@ -255,29 +274,52 @@ def tile_variableselectionnetwork_pb_t_kernel(
                     start=False,
                     stop=(c == CHUNKS - 1),
                 )
-            r = norm.tile([P, D], F32, tag="r")
-            if k == TOTAL - 1:
-                nc.scalar.copy(out=r[:], in_=r_ps[:])
-                moments = stat.tile([P, 6], F32, tag="moments")
-                nc.vector.bn_stats(out=moments[:], in_=r[:])
-                nc.vector.bn_aggr(out=tiles["mean_var", k][:, i, :], in_=moments[:])
+            if k == LAST:
+                tiles["r%d" % i, k] = r_ps
             else:
+                r = norm.tile([P, D], F32, tag="r")
                 nc.scalar.activation(
                     out=r[:], in_=r_ps[:], func=ACT.Identity, accum_out=tiles["row_sum", k][:, i : i + 1]
                 )
-            tiles["r%d" % i, k] = r
+                tiles["r%d" % i, k] = r
 
-        def last_statistics(k):
-            neg_mean = stat.tile([P, UNIT_TILES], F32, tag="neg_mean")
-            nc.vector.tensor_scalar(
-                out=neg_mean[:], in0=tiles["mean_var", k][:, :, 0], scalar1=-1.0, scalar2=None, op0=ALU.mult
-            )
+        def last_moments(i):
+            moments = stat.tile([P, 6], F32, tag="moments")
+            nc.vector.bn_stats(out=moments[:], in_=tiles["r%d" % i, LAST][:])
+            nc.vector.bn_aggr(out=tiles["mean_var", LAST][:, i, :], in_=moments[:])
+
+        def last_deviation():
             var_eps = stat.tile([P, UNIT_TILES], F32, tag="var_eps")
             nc.vector.tensor_scalar(
-                out=var_eps[:], in0=tiles["mean_var", k][:, :, 1], scalar1=EPS, scalar2=None, op0=ALU.add
+                out=var_eps[:], in0=tiles["mean_var", LAST][:, :, 1], scalar1=EPS, scalar2=None, op0=ALU.add
             )
-            tiles["neg_mean", k] = neg_mean
-            tiles["var_eps", k] = var_eps
+            rstd = stat.tile([P, UNIT_TILES], F32, tag="rstd")
+            nc.gpsimd.tensor_tensor(out=rstd[:], in0=var_eps[:], in1=neg_half[:], op=ALU.pow)
+            tiles["rstd", LAST] = rstd
+            z = gate.tile([P, UNIT_TILES, D], F32, tag="z", bufs=2)
+            tiles["z", LAST] = z
+
+        def last_gain(i):
+            nc.vector.scalar_tensor_tensor(
+                out=tiles["z", LAST][:, i, :],
+                in0=tiles["r%d" % i, LAST][:],
+                scalar=tiles["mean_var", LAST][:, i, 0:1],
+                in1=gs_spread[:, 0, :],
+                op0=ALU.subtract,
+                op1=ALU.mult,
+            )
+
+        def last_shift(i):
+            z = tiles["z", LAST][:, i, :]
+            nc.vector.scalar_tensor_tensor(
+                out=z, in0=z, scalar=tiles["rstd", LAST][:, i : i + 1], in1=gs_spread[:, 1, :],
+                op0=ALU.mult, op1=ALU.add,
+            )
+
+        def last_weigh(i):
+            z = tiles["z", LAST][:, i, :]
+            nc.vector.tensor_tensor(out=z, in0=z, in1=tiles["sel_u", LAST][:, i, :], op=ALU.mult)
+            tiles["product%d" % i, LAST] = z
 
         def mean(k):
             neg_mean = stat.tile([P, UNIT_TILES], F32, tag="neg_mean")
@@ -301,20 +343,24 @@ def tile_variableselectionnetwork_pb_t_kernel(
             tiles["var_eps", k] = var_eps
 
         def normalise(k):
-            rstd = stat.tile([P, UNIT_TILES], F32, tag="rstd")
-            nc.gpsimd.tensor_tensor(out=rstd[:], in0=tiles["var_eps", k][:], in1=neg_half[:], op=ALU.pow)
-            z = gate.tile([P, UNIT_TILES, D], F32, tag="z", bufs=2)
             for i in range(UNIT_TILES):
-                engine = nc.vector if k == TOTAL - 1 else nc.gpsimd
-                engine.tensor_scalar(
-                    out=z[:, i, :],
-                    in0=tiles["r%d" % i, k][:],
-                    scalar1=tiles["neg_mean", k][:, i : i + 1],
-                    scalar2=rstd[:, i : i + 1],
-                    op0=ALU.add,
-                    op1=ALU.mult,
-                )
-            tiles["z", k] = z
+                normalise_tile(k, i)
+
+        def normalise_tile(k, i):
+            if i == 0:
+                rstd = stat.tile([P, UNIT_TILES], F32, tag="rstd")
+                nc.gpsimd.tensor_tensor(out=rstd[:], in0=tiles["var_eps", k][:], in1=neg_half[:], op=ALU.pow)
+                z = gate.tile([P, UNIT_TILES, D], F32, tag="z", bufs=2)
+                tiles["rstd", k] = rstd
+                tiles["z", k] = z
+            nc.gpsimd.tensor_scalar(
+                out=tiles["z", k][:, i, :],
+                in0=tiles["r%d" % i, k][:],
+                scalar1=tiles["neg_mean", k][:, i : i + 1],
+                scalar2=tiles["rstd", k][:, i : i + 1],
+                op0=ALU.add,
+                op1=ALU.mult,
+            )
 
         def gain_shift(k, chunks):
             n = k // UNITS
@@ -330,12 +376,7 @@ def tile_variableselectionnetwork_pb_t_kernel(
                     )
                 gain = gs_cols[:, c, n : n + 1]
                 shift = gs_cols[:, c, VARS + n : VARS + n + 1]
-                if k in (TOTAL - 3, TOTAL - 1) and c % 2 == 1:
-                    nc.vector.tensor_scalar(
-                        out=y[:, c, :], in0=z_ps[:], scalar1=gain, scalar2=shift, op0=ALU.mult, op1=ALU.add
-                    )
-                else:
-                    nc.scalar.activation(out=y[:, c, :], in_=z_ps[:], func=ACT.Identity, bias=shift, scale=gain)
+                nc.scalar.activation(out=y[:, c, :], in_=z_ps[:], func=ACT.Identity, bias=shift, scale=gain)
 
         def weigh(k, i):
             y_ps = psum.tile([P, D], F32, tag="to_vector", bufs=VECTOR_BANKS)
@@ -354,7 +395,7 @@ def tile_variableselectionnetwork_pb_t_kernel(
         def accumulate(k, i):
             tile_no = k % UNITS * UNIT_TILES + i
             total = acc[:, tile_no, :]
-            adder = nc.vector if k == TOTAL - 1 or (k == TOTAL - 2 and i > 0) else nc.gpsimd
+            adder = nc.vector if (k, i) in ADD_BY_VECTOR else nc.gpsimd
             adder.tensor_tensor(out=total, in0=total, in1=tiles["product%d" % i, k], op=ALU.add)
             if k // UNITS == VARS - 1:
                 nc.sync.dma_start(out=out[tile_no * P : (tile_no + 1) * P, :], in_=total)
@@ -362,7 +403,7 @@ def tile_variableselectionnetwork_pb_t_kernel(
         def weights_at(late, early):
             return [m for m in range(3 * VARS) if (step == early[m] if m < 3 else m == late)]
 
-        for step in range(-4, TOTAL):
+        for step in range(-4, LAST):
             for m in weights_at(step + 6, (-4, -4, -4)):
                 if m != 1 and m != 2:
                     weight_load(m)
@@ -406,27 +447,40 @@ def tile_variableselectionnetwork_pb_t_kernel(
             if live(step + 3):
                 hv_transpose(step + 3, 0)
                 hv_transpose(step + 3, 1)
-            if live(step) and step == TOTAL - 1:
-                last_statistics(step)
-            elif live(step):
+            if live(step):
                 mean(step)
-            if live(step - 2) and (step - 2) // UNITS > 0 and step < TOTAL - 1:
+            if live(step - 2) and (step - 2) // UNITS > 0:
                 for i in range(UNIT_TILES):
                     accumulate(step - 2, i)
             if step == -3:
                 column_constants()
 
-        normalise(TOTAL - 1)
-        gain_shift(TOTAL - 2, range(CHUNKS))
+        load_sel(LAST)
+        gate_layers(LAST)
+        squares(LAST - 1)
+        gain_shift(LAST - 2, range(CHUNKS))
         for i in range(UNIT_TILES):
-            weigh(TOTAL - 2, i)
-        gain_shift(TOTAL - 1, range(CHUNKS))
-        accumulate(TOTAL - 2, 0)
+            residual(LAST, i)
+            last_moments(i)
+        for i in range(2):
+            normalise_tile(LAST - 1, i)
+        last_deviation()
+        for i in range(2, UNIT_TILES):
+            normalise_tile(LAST - 1, i)
         for i in range(UNIT_TILES):
-            accumulate(TOTAL - 3, i)
+            last_gain(i)
         for i in range(UNIT_TILES):
-            weigh(TOTAL - 1, i)
-        for i in range(1, UNIT_TILES):
-            accumulate(TOTAL - 2, i)
+            weigh(LAST - 2, i)
         for i in range(UNIT_TILES):
-            accumulate(TOTAL - 1, i)
+            last_shift(i)
+        gain_shift(LAST - 1, range(CHUNKS))
+        for i in range(UNIT_TILES):
+            accumulate(LAST - 2, i)
+        for i in range(UNIT_TILES):
+            weigh(LAST - 1, i)
+        for i in range(UNIT_TILES):
+            accumulate(LAST - 1, i)
+        for i in range(UNIT_TILES):
+            last_weigh(i)
+        for i in range(UNIT_TILES):
+            accumulate(LAST, i)

@@ -24,7 +24,7 @@ TOTAL = VARS * UNITS
 EPS = 1e-5
 EARLY = 3
 LAST = TOTAL - 1
-ADD_BY_VECTOR = [(k, i) for k in range(TOTAL - 3, TOTAL) for i in range(UNIT_TILES)]
+ADD_BY_VECTOR = [(LAST - 1, 3)] + [(LAST, i) for i in range(UNIT_TILES)]
 SCALAR_BANKS, VECTOR_BANKS = 4, 4
 
 FLOPS = 3 * VARS * 2 * BATCH * D * D
@@ -52,6 +52,8 @@ def tile_variableselectionnetwork_pb_t_kernel(
         make_identity(nc, ident_b[:])
         neg_half = const.tile([P, UNIT_TILES], F32)
         nc.vector.memset(neg_half[:], -0.5)
+        unread_sigmoid = const.tile([P, UNIT_TILES], F32)
+        nc.scalar.activation(out=unread_sigmoid[:], in_=neg_half[:], func=ACT.Sigmoid)
 
         vb1_cols = const.tile([P, VARS, CHUNKS], BF16)
         nc.scalar.dma_start(out=vb1_cols[:], in_=vb1.rearrange("n (p c) -> p n c", c=CHUNKS))
@@ -71,7 +73,7 @@ def tile_variableselectionnetwork_pb_t_kernel(
 
         bias_cols = const.tile([P, 2, VARS, CHUNKS], F32)
         gs_cols = const.tile([P, CHUNKS, 2 * VARS], F32)
-        gs_spread = const.tile([P, 2, D], BF16)
+        gain_spread = const.tile([P, D], BF16)
 
         tiles = {}
 
@@ -133,17 +135,14 @@ def tile_variableselectionnetwork_pb_t_kernel(
             for c in range(CHUNKS):
                 nc.tensor.transpose(gs_ps[:, c, :], gs_rows[:, c * P : (c + 1) * P], ident_b[:])
             nc.scalar.copy(out=gs_cols[:], in_=gs_ps[:, :, 0 : 2 * VARS])
-            spread_ps = psum.tile([P, 2, D], BF16, tag="to_scalar")
-            for v in range(2):
-                row = v * VARS + VARS - 1
-                nc.tensor.matmul(
-                    out=spread_ps[:, v, :],
-                    lhsT=ident_b[:, row : row + 1].to_broadcast([P, P]),
-                    rhs=gs_rows[:],
-                    start=True,
-                    stop=True,
-                )
-            nc.scalar.copy(out=gs_spread[:], in_=spread_ps[:])
+            gain_ps = psum.tile([P, D], BF16, tag="to_scalar")
+            spread(VARS - 1, gain_ps)
+            nc.scalar.copy(out=gain_spread[:], in_=gain_ps[:])
+
+        def spread(row, to_ps):
+            nc.tensor.matmul(
+                out=to_ps[:], lhsT=ident_b[:, row : row + 1].to_broadcast([P, P]), rhs=gs_rows[:], start=True, stop=True
+            )
 
         def unit_rows(dram, k):
             first = (k % UNITS) * UNIT_ROWS
@@ -304,21 +303,33 @@ def tile_variableselectionnetwork_pb_t_kernel(
                 out=tiles["z", LAST][:, i, :],
                 in0=tiles["r%d" % i, LAST][:],
                 scalar=tiles["mean_var", LAST][:, i, 0:1],
-                in1=gs_spread[:, 0, :],
+                in1=gain_spread[:],
                 op0=ALU.subtract,
                 op1=ALU.mult,
             )
 
+        def last_shift_to_psum():
+            shift_ps = psum.tile([P, D], BF16, tag="to_vector", bufs=VECTOR_BANKS)
+            spread(2 * VARS - 1, shift_ps)
+            tiles["shift", LAST] = shift_ps
+
+        def last_sel_to_psum(i):
+            sel_ps = psum.tile([P, D], F32, tag="to_vector", bufs=VECTOR_BANKS)
+            nc.tensor.matmul(
+                out=sel_ps[:], lhsT=ident_b[:], rhs=tiles["sel_u", LAST][:, i, :], start=True, stop=True
+            )
+            tiles["sel_ps%d" % i, LAST] = sel_ps
+
         def last_shift(i):
             z = tiles["z", LAST][:, i, :]
             nc.vector.scalar_tensor_tensor(
-                out=z, in0=z, scalar=tiles["rstd", LAST][:, i : i + 1], in1=gs_spread[:, 1, :],
+                out=z, in0=z, scalar=tiles["rstd", LAST][:, i : i + 1], in1=tiles["shift", LAST][:],
                 op0=ALU.mult, op1=ALU.add,
             )
 
         def last_weigh(i):
             z = tiles["z", LAST][:, i, :]
-            nc.vector.tensor_tensor(out=z, in0=z, in1=tiles["sel_u", LAST][:, i, :], op=ALU.mult)
+            nc.vector.tensor_tensor(out=z, in0=z, in1=tiles["sel_ps%d" % i, LAST][:], op=ALU.mult)
             tiles["product%d" % i, LAST] = z
 
         def mean(k):
@@ -400,22 +411,40 @@ def tile_variableselectionnetwork_pb_t_kernel(
             if k // UNITS == VARS - 1:
                 nc.sync.dma_start(out=out[tile_no * P : (tile_no + 1) * P, :], in_=total)
 
-        def weights_at(late, early):
-            return [m for m in range(3 * VARS) if (step == early[m] if m < 3 else m == late)]
+        load_hv(0)
+        for m in range(3):
+            weight_load(m)
+        load_hv(1)
+        load_x(0)
+        load_hv(2)
+        weight_load(3)
+        weight_regroup(0)
+        hv_transpose(0, 0)
+        hv_transpose(0, 1)
+        weight_quantise(0)
+        hv_quantise(0)
+        weight_regroup(1)
+        weight_regroup(2)
+        for i in range(UNIT_TILES):
+            first_layer(0, i)
+        hv_transpose(1, 0)
+        hv_transpose(1, 1)
+        column_constants()
+        hv_transpose(2, 0)
+        hv_transpose(2, 1)
+        weight_quantise(1)
+        weight_quantise(2)
+        e1_quantise(0)
+        hv_quantise(1)
 
-        for step in range(-4, LAST):
-            for m in weights_at(step + 6, (-4, -4, -4)):
-                if m != 1 and m != 2:
-                    weight_load(m)
-            if live(step + 4):
-                load_hv(step + 4)
-            if step == -4:
-                weight_load(1)
-                weight_load(2)
+        for step in range(LAST):
+            if live(step + 3):
+                load_hv(step + 3)
             if live(step + 1):
                 load_x(step + 1)
-            if live(step):
-                load_sel(step)
+            load_sel(step)
+            if step + 4 < 3 * VARS:
+                weight_load(step + 4)
 
             if live(step):
                 gate_layers(step)
@@ -428,12 +457,12 @@ def tile_variableselectionnetwork_pb_t_kernel(
             if live(step + 1):
                 for i in range(1, UNIT_TILES):
                     first_layer(step + 1, i)
-            for m in weights_at(step + 4, (-4, -3, -3)):
-                weight_regroup(m)
+            if step + 3 < 3 * VARS:
+                weight_regroup(step + 3)
             if live(step + 1):
                 e1_quantise(step + 1)
-            for m in weights_at(step + 3, (-4, -3, -3)):
-                weight_quantise(m)
+            if step + 3 < 3 * VARS:
+                weight_quantise(step + 3)
             if live(step + 2):
                 hv_quantise(step + 2)
             if live(step - 1):
@@ -447,13 +476,10 @@ def tile_variableselectionnetwork_pb_t_kernel(
             if live(step + 3):
                 hv_transpose(step + 3, 0)
                 hv_transpose(step + 3, 1)
-            if live(step):
-                mean(step)
+            mean(step)
             if live(step - 2) and (step - 2) // UNITS > 0:
                 for i in range(UNIT_TILES):
                     accumulate(step - 2, i)
-            if step == -3:
-                column_constants()
 
         load_sel(LAST)
         gate_layers(LAST)
@@ -472,15 +498,17 @@ def tile_variableselectionnetwork_pb_t_kernel(
         for i in range(UNIT_TILES):
             weigh(LAST - 2, i)
         for i in range(UNIT_TILES):
+            accumulate(LAST - 2, i)
+        last_shift_to_psum()
+        for i in range(UNIT_TILES):
             last_shift(i)
         gain_shift(LAST - 1, range(CHUNKS))
-        for i in range(UNIT_TILES):
-            accumulate(LAST - 2, i)
         for i in range(UNIT_TILES):
             weigh(LAST - 1, i)
         for i in range(UNIT_TILES):
             accumulate(LAST - 1, i)
         for i in range(UNIT_TILES):
+            last_sel_to_psum(i)
             last_weigh(i)
         for i in range(UNIT_TILES):
             accumulate(LAST, i)

@@ -24,7 +24,7 @@ TOTAL = VARS * UNITS
 EPS = 1e-5
 EARLY = 3
 LAST = TOTAL - 1
-ADD_BY_VECTOR = [(LAST - 1, 3)] + [(LAST, i) for i in range(UNIT_TILES)]
+ADD_BY_VECTOR = [(LAST - 1, i) for i in range(1, UNIT_TILES)]
 SCALAR_BANKS, VECTOR_BANKS = 4, 4
 
 FLOPS = 3 * VARS * 2 * BATCH * D * D
@@ -73,7 +73,8 @@ def tile_variableselectionnetwork_pb_t_kernel(
 
         bias_cols = const.tile([P, 2, VARS, CHUNKS], F32)
         gs_cols = const.tile([P, CHUNKS, 2 * VARS], F32)
-        gain_spread = const.tile([P, D], BF16)
+        gs_spread = const.tile([P, 2, D], BF16)
+        sel_gain = const.tile([P, UNIT_TILES, D], F32)
 
         tiles = {}
 
@@ -135,13 +136,29 @@ def tile_variableselectionnetwork_pb_t_kernel(
             for c in range(CHUNKS):
                 nc.tensor.transpose(gs_ps[:, c, :], gs_rows[:, c * P : (c + 1) * P], ident_b[:])
             nc.scalar.copy(out=gs_cols[:], in_=gs_ps[:, :, 0 : 2 * VARS])
-            gain_ps = psum.tile([P, D], BF16, tag="to_scalar")
-            spread(VARS - 1, gain_ps)
-            nc.scalar.copy(out=gain_spread[:], in_=gain_ps[:])
+            spread_ps = psum.tile([P, 2, D], BF16, tag="to_scalar")
+            for v in range(2):
+                row = v * VARS + VARS - 1
+                nc.tensor.matmul(
+                    out=spread_ps[:, v, :],
+                    lhsT=ident_b[:, row : row + 1].to_broadcast([P, P]),
+                    rhs=gs_rows[:],
+                    start=True,
+                    stop=True,
+                )
+            nc.scalar.copy(out=gs_spread[:], in_=spread_ps[:])
 
-        def spread(row, to_ps):
-            nc.tensor.matmul(
-                out=to_ps[:], lhsT=ident_b[:, row : row + 1].to_broadcast([P, P]), rhs=gs_rows[:], start=True, stop=True
+        def last_sel_gain(i):
+            nc.gpsimd.tensor_tensor(
+                out=sel_gain[:, i, :], in0=tiles["sel_u", LAST][:, i, :], in1=gs_spread[:, 0, :], op=ALU.mult
+            )
+
+        def last_sel_shift(i):
+            nc.gpsimd.tensor_tensor(
+                out=acc[:, LAST % UNITS * UNIT_TILES + i, :],
+                in0=tiles["sel_u", LAST][:, i, :],
+                in1=gs_spread[:, 1, :],
+                op=ALU.mult,
             )
 
         def unit_rows(dram, k):
@@ -159,7 +176,8 @@ def tile_variableselectionnetwork_pb_t_kernel(
             tiles["x_u", k] = x_u
 
         def load_sel(k):
-            sel_u = loads.tile([P, UNIT_TILES, D], BF16, tag="sel_u", bufs=3)
+            pool, tag, bufs = (const, "sel_last", 1) if k == LAST else (loads, "sel_u", 3)
+            sel_u = pool.tile([P, UNIT_TILES, D], BF16, tag=tag, bufs=bufs)
             nc.sync.dma_start(out=sel_u[:], in_=unit_rows(sel_w, k))
             tiles["sel_u", k] = sel_u
 
@@ -298,39 +316,28 @@ def tile_variableselectionnetwork_pb_t_kernel(
             z = gate.tile([P, UNIT_TILES, D], F32, tag="z", bufs=2)
             tiles["z", LAST] = z
 
-        def last_gain(i):
+        def last_centre(i):
             nc.vector.scalar_tensor_tensor(
                 out=tiles["z", LAST][:, i, :],
                 in0=tiles["r%d" % i, LAST][:],
                 scalar=tiles["mean_var", LAST][:, i, 0:1],
-                in1=gain_spread[:],
+                in1=sel_gain[:, i, :],
                 op0=ALU.subtract,
                 op1=ALU.mult,
             )
 
-        def last_shift_to_psum():
-            shift_ps = psum.tile([P, D], BF16, tag="to_vector", bufs=VECTOR_BANKS)
-            spread(2 * VARS - 1, shift_ps)
-            tiles["shift", LAST] = shift_ps
-
-        def last_sel_to_psum(i):
-            sel_ps = psum.tile([P, D], F32, tag="to_vector", bufs=VECTOR_BANKS)
-            nc.tensor.matmul(
-                out=sel_ps[:], lhsT=ident_b[:], rhs=tiles["sel_u", LAST][:, i, :], start=True, stop=True
-            )
-            tiles["sel_ps%d" % i, LAST] = sel_ps
-
-        def last_shift(i):
-            z = tiles["z", LAST][:, i, :]
+        def last_finish(i):
+            tile_no = LAST % UNITS * UNIT_TILES + i
+            total = acc[:, tile_no, :]
             nc.vector.scalar_tensor_tensor(
-                out=z, in0=z, scalar=tiles["rstd", LAST][:, i : i + 1], in1=tiles["shift", LAST][:],
-                op0=ALU.mult, op1=ALU.add,
+                out=total,
+                in0=tiles["z", LAST][:, i, :],
+                scalar=tiles["rstd", LAST][:, i : i + 1],
+                in1=total,
+                op0=ALU.mult,
+                op1=ALU.add,
             )
-
-        def last_weigh(i):
-            z = tiles["z", LAST][:, i, :]
-            nc.vector.tensor_tensor(out=z, in0=z, in1=tiles["sel_ps%d" % i, LAST][:], op=ALU.mult)
-            tiles["product%d" % i, LAST] = z
+            nc.sync.dma_start(out=out[tile_no * P : (tile_no + 1) * P, :], in_=total)
 
         def mean(k):
             neg_mean = stat.tile([P, UNIT_TILES], F32, tag="neg_mean")
@@ -395,10 +402,10 @@ def tile_variableselectionnetwork_pb_t_kernel(
                 nc.tensor.transpose(
                     y_ps[:, c * P : (c + 1) * P], tiles["y", k][:, c, i * P : (i + 1) * P], ident_f[:]
                 )
-            if k // UNITS == 0:
+            if k // UNITS == 0 and k != LAST % UNITS:
                 product = acc[:, k % UNITS * UNIT_TILES + i, :]
             else:
-                product_tile = norm.tile([P, D], F32, tag="product")
+                product_tile = norm.tile([P, D], F32, tag="product", bufs=6)
                 product = product_tile[:]
             nc.vector.tensor_tensor(out=product, in0=y_ps[:], in1=tiles["sel_u", k][:, i, :], op=ALU.mult)
             tiles["product%d" % i, k] = product
@@ -418,6 +425,7 @@ def tile_variableselectionnetwork_pb_t_kernel(
         load_x(0)
         load_hv(2)
         weight_load(3)
+        load_sel(LAST)
         weight_regroup(0)
         hv_transpose(0, 0)
         hv_transpose(0, 1)
@@ -477,38 +485,39 @@ def tile_variableselectionnetwork_pb_t_kernel(
                 hv_transpose(step + 3, 0)
                 hv_transpose(step + 3, 1)
             mean(step)
-            if live(step - 2) and (step - 2) // UNITS > 0:
+            if step == 1:
+                last_sel_shift(0)
+                last_sel_shift(1)
+                last_sel_shift(2)
+            if step == 2:
+                last_sel_shift(3)
+                last_sel_gain(0)
+                last_sel_gain(1)
+            if step == 3:
+                last_sel_gain(2)
+                last_sel_gain(3)
+            if live(step - 2) and (step - 2 >= UNITS or step - 2 == LAST % UNITS):
                 for i in range(UNIT_TILES):
                     accumulate(step - 2, i)
 
-        load_sel(LAST)
         gate_layers(LAST)
         squares(LAST - 1)
+        normalise(LAST - 1)
         gain_shift(LAST - 2, range(CHUNKS))
         for i in range(UNIT_TILES):
             residual(LAST, i)
             last_moments(i)
-        for i in range(2):
-            normalise_tile(LAST - 1, i)
         last_deviation()
-        for i in range(2, UNIT_TILES):
-            normalise_tile(LAST - 1, i)
         for i in range(UNIT_TILES):
-            last_gain(i)
+            last_centre(i)
         for i in range(UNIT_TILES):
             weigh(LAST - 2, i)
         for i in range(UNIT_TILES):
             accumulate(LAST - 2, i)
-        last_shift_to_psum()
-        for i in range(UNIT_TILES):
-            last_shift(i)
         gain_shift(LAST - 1, range(CHUNKS))
         for i in range(UNIT_TILES):
             weigh(LAST - 1, i)
         for i in range(UNIT_TILES):
+            last_finish(i)
+        for i in range(UNIT_TILES):
             accumulate(LAST - 1, i)
-        for i in range(UNIT_TILES):
-            last_sel_to_psum(i)
-            last_weigh(i)
-        for i in range(UNIT_TILES):
-            accumulate(LAST, i)

@@ -24,7 +24,8 @@ TOTAL = VARS * UNITS
 EPS = 1e-5
 EARLY = 3
 LAST = TOTAL - 1
-ADD_BY_VECTOR = [(LAST - 1, i) for i in range(1, UNIT_TILES)]
+LAST_BY_VECTOR = 2
+DIRECT = (LAST - 1, LAST)
 SCALAR_BANKS, VECTOR_BANKS = 4, 4
 
 FLOPS = 3 * VARS * 2 * BATCH * D * D
@@ -74,7 +75,7 @@ def tile_variableselectionnetwork_pb_t_kernel(
         bias_cols = const.tile([P, 2, VARS, CHUNKS], F32)
         gs_cols = const.tile([P, CHUNKS, 2 * VARS], F32)
         gs_spread = const.tile([P, 2, D], BF16)
-        sel_gain = const.tile([P, UNIT_TILES, D], F32)
+        sel_gain = const.tile([P, len(DIRECT) * UNIT_TILES, D], F32)
 
         tiles = {}
 
@@ -83,7 +84,7 @@ def tile_variableselectionnetwork_pb_t_kernel(
 
         def weight_load(m):
             n = m // 3
-            raw = wstage.tile([P, PACK, D], BF16, tag="w_raw", bufs=5)
+            raw = wstage.tile([P, PACK, D], BF16, tag="w_raw", bufs=4)
             w = (vW1, vW4, vW5)[m % 3]
             nc.sync.dma_start(out=raw[:], in_=w[n].rearrange("(p t) c -> p t c", t=PACK))
             tiles["w_raw", m] = raw
@@ -148,15 +149,19 @@ def tile_variableselectionnetwork_pb_t_kernel(
                 )
             nc.scalar.copy(out=gs_spread[:], in_=spread_ps[:])
 
-        def last_sel_gain(i):
-            nc.gpsimd.tensor_tensor(
-                out=sel_gain[:, i, :], in0=tiles["sel_u", LAST][:, i, :], in1=gs_spread[:, 0, :], op=ALU.mult
+        def sel_gain_of(k, i):
+            return sel_gain[:, DIRECT.index(k) * UNIT_TILES + i, :]
+
+        def sel_times_gain(k, i):
+            engine = nc.vector if k == LAST else nc.gpsimd
+            engine.tensor_tensor(
+                out=sel_gain_of(k, i), in0=tiles["sel_u", k][:, i, :], in1=gs_spread[:, 0, :], op=ALU.mult
             )
 
-        def last_sel_shift(i):
+        def sel_times_shift(k, i):
             nc.gpsimd.tensor_tensor(
-                out=acc[:, LAST % UNITS * UNIT_TILES + i, :],
-                in0=tiles["sel_u", LAST][:, i, :],
+                out=acc[:, k % UNITS * UNIT_TILES + i, :],
+                in0=tiles["sel_u", k][:, i, :],
                 in1=gs_spread[:, 1, :],
                 op=ALU.mult,
             )
@@ -176,8 +181,10 @@ def tile_variableselectionnetwork_pb_t_kernel(
             tiles["x_u", k] = x_u
 
         def load_sel(k):
-            pool, tag, bufs = (const, "sel_last", 1) if k == LAST else (loads, "sel_u", 3)
-            sel_u = pool.tile([P, UNIT_TILES, D], BF16, tag=tag, bufs=bufs)
+            direct = k in DIRECT
+            sel_u = loads.tile(
+                [P, UNIT_TILES, D], BF16, tag="sel_direct" if direct else "sel_u", bufs=len(DIRECT) if direct else 3
+            )
             nc.sync.dma_start(out=sel_u[:], in_=unit_rows(sel_w, k))
             tiles["sel_u", k] = sel_u
 
@@ -268,19 +275,14 @@ def tile_variableselectionnetwork_pb_t_kernel(
                 )
             tiles["gv_t", k] = gv_t
 
+        def by_scalar_from(k):
+            return LAST_BY_VECTOR if k == LAST else 0
+
         def residual(k, i):
-            if i == 0 and k == TOTAL - 1:
-                mean_var = stat.tile([P, UNIT_TILES, 2], F32, tag="mean_var")
-                tiles["mean_var", k] = mean_var
-            elif i == 0:
+            if i == 0:
                 row_sum = stat.tile([P, UNIT_TILES], F32, tag="row_sum")
                 tiles["row_sum", k] = row_sum
-            r_ps = psum.tile(
-                [P, D],
-                F32,
-                tag="to_vector" if k == LAST else "to_scalar",
-                bufs=VECTOR_BANKS if k == LAST else SCALAR_BANKS,
-            )
+            r_ps = psum.tile([P, D], F32, tag="to_scalar")
             nc.tensor.matmul(out=r_ps[:], lhsT=ident_b[:], rhs=tiles["x_u", k][:, i, :], start=True, stop=False)
             for c in range(CHUNKS):
                 nc.tensor.matmul(
@@ -291,48 +293,55 @@ def tile_variableselectionnetwork_pb_t_kernel(
                     start=False,
                     stop=(c == CHUNKS - 1),
                 )
-            if k == LAST:
-                tiles["r%d" % i, k] = r_ps
-            else:
+            tiles["r_ps%d" % i, k] = r_ps
+            if i >= by_scalar_from(k):
                 r = norm.tile([P, D], F32, tag="r")
                 nc.scalar.activation(
                     out=r[:], in_=r_ps[:], func=ACT.Identity, accum_out=tiles["row_sum", k][:, i : i + 1]
                 )
                 tiles["r%d" % i, k] = r
 
-        def last_moments(i):
-            moments = stat.tile([P, 6], F32, tag="moments")
-            nc.vector.bn_stats(out=moments[:], in_=tiles["r%d" % i, LAST][:])
-            nc.vector.bn_aggr(out=tiles["mean_var", LAST][:, i, :], in_=moments[:])
-
-        def last_deviation():
-            var_eps = stat.tile([P, UNIT_TILES], F32, tag="var_eps")
+        def last_moments():
+            mean_var = stat.tile([P, LAST_BY_VECTOR, 2], F32, tag="mean_var")
+            for i in range(LAST_BY_VECTOR):
+                moments = stat.tile([P, 6], F32, tag="moments")
+                nc.vector.bn_stats(out=moments[:], in_=tiles["r_ps%d" % i, LAST][:])
+                nc.vector.bn_aggr(out=mean_var[:, i, :], in_=moments[:])
+            tiles["mean_var", LAST] = mean_var
             nc.vector.tensor_scalar(
-                out=var_eps[:], in0=tiles["mean_var", LAST][:, :, 1], scalar1=EPS, scalar2=None, op0=ALU.add
+                out=tiles["var_eps", LAST][:, 0:LAST_BY_VECTOR],
+                in0=mean_var[:, :, 1],
+                scalar1=EPS,
+                scalar2=None,
+                op0=ALU.add,
             )
-            rstd = stat.tile([P, UNIT_TILES], F32, tag="rstd")
-            nc.gpsimd.tensor_tensor(out=rstd[:], in0=var_eps[:], in1=neg_half[:], op=ALU.pow)
-            tiles["rstd", LAST] = rstd
-            z = gate.tile([P, UNIT_TILES, D], F32, tag="z", bufs=2)
-            tiles["z", LAST] = z
 
-        def last_centre(i):
+        def inverse_deviation(k):
+            rstd = stat.tile([P, UNIT_TILES], F32, tag="rstd")
+            nc.gpsimd.tensor_tensor(out=rstd[:], in0=tiles["var_eps", k][:], in1=neg_half[:], op=ALU.pow)
+            tiles["rstd", k] = rstd
+
+        def centre(k, i):
+            if i == 0:
+                z = gate.tile([P, UNIT_TILES, D], F32, tag="z", bufs=2)
+                tiles["z", k] = z
+            by_scalar = i >= by_scalar_from(k)
             nc.vector.scalar_tensor_tensor(
-                out=tiles["z", LAST][:, i, :],
-                in0=tiles["r%d" % i, LAST][:],
-                scalar=tiles["mean_var", LAST][:, i, 0:1],
-                in1=sel_gain[:, i, :],
-                op0=ALU.subtract,
+                out=tiles["z", k][:, i, :],
+                in0=tiles[("r_ps%d" if k == LAST else "r%d") % i, k][:],
+                scalar=tiles["neg_mean", k][:, i : i + 1] if by_scalar else tiles["mean_var", k][:, i, 0:1],
+                in1=sel_gain_of(k, i),
+                op0=ALU.add if by_scalar else ALU.subtract,
                 op1=ALU.mult,
             )
 
-        def last_finish(i):
-            tile_no = LAST % UNITS * UNIT_TILES + i
+        def finish(k, i):
+            tile_no = k % UNITS * UNIT_TILES + i
             total = acc[:, tile_no, :]
             nc.vector.scalar_tensor_tensor(
                 out=total,
-                in0=tiles["z", LAST][:, i, :],
-                scalar=tiles["rstd", LAST][:, i : i + 1],
+                in0=tiles["z", k][:, i, :],
+                scalar=tiles["rstd", k][:, i : i + 1],
                 in1=total,
                 op0=ALU.mult,
                 op1=ALU.add,
@@ -341,12 +350,13 @@ def tile_variableselectionnetwork_pb_t_kernel(
 
         def mean(k):
             neg_mean = stat.tile([P, UNIT_TILES], F32, tag="neg_mean")
-            nc.scalar.mul(out=neg_mean[:], in_=tiles["row_sum", k][:], mul=-1.0 / D)
+            cols = slice(by_scalar_from(k), UNIT_TILES)
+            nc.scalar.mul(out=neg_mean[:, cols], in_=tiles["row_sum", k][:, cols], mul=-1.0 / D)
             tiles["neg_mean", k] = neg_mean
 
         def squares(k):
             sq_sum = stat.tile([P, UNIT_TILES], F32, tag="sq_sum")
-            for i in range(UNIT_TILES):
+            for i in range(by_scalar_from(k), UNIT_TILES):
                 sq = norm.tile([P, D], BF16, tag="squares", bufs=4)
                 nc.scalar.activation(
                     out=sq[:],
@@ -357,7 +367,8 @@ def tile_variableselectionnetwork_pb_t_kernel(
                     accum_out=sq_sum[:, i : i + 1],
                 )
             var_eps = stat.tile([P, UNIT_TILES], F32, tag="var_eps")
-            nc.scalar.activation(out=var_eps[:], in_=sq_sum[:], func=ACT.Copy, bias=EPS, scale=1.0 / D)
+            cols = slice(by_scalar_from(k), UNIT_TILES)
+            nc.scalar.activation(out=var_eps[:, cols], in_=sq_sum[:, cols], func=ACT.Copy, bias=EPS, scale=1.0 / D)
             tiles["var_eps", k] = var_eps
 
         def normalise(k):
@@ -394,7 +405,12 @@ def tile_variableselectionnetwork_pb_t_kernel(
                     )
                 gain = gs_cols[:, c, n : n + 1]
                 shift = gs_cols[:, c, VARS + n : VARS + n + 1]
-                nc.scalar.activation(out=y[:, c, :], in_=z_ps[:], func=ACT.Identity, bias=shift, scale=gain)
+                if k >= LAST - 4 and c == CHUNKS - 1:
+                    nc.vector.tensor_scalar(
+                        out=y[:, c, :], in0=z_ps[:], scalar1=gain, scalar2=shift, op0=ALU.mult, op1=ALU.add
+                    )
+                else:
+                    nc.scalar.activation(out=y[:, c, :], in_=z_ps[:], func=ACT.Identity, bias=shift, scale=gain)
 
         def weigh(k, i):
             y_ps = psum.tile([P, D], F32, tag="to_vector", bufs=VECTOR_BANKS)
@@ -402,7 +418,7 @@ def tile_variableselectionnetwork_pb_t_kernel(
                 nc.tensor.transpose(
                     y_ps[:, c * P : (c + 1) * P], tiles["y", k][:, c, i * P : (i + 1) * P], ident_f[:]
                 )
-            if k // UNITS == 0 and k != LAST % UNITS:
+            if k == 0:
                 product = acc[:, k % UNITS * UNIT_TILES + i, :]
             else:
                 product_tile = norm.tile([P, D], F32, tag="product", bufs=6)
@@ -413,10 +429,10 @@ def tile_variableselectionnetwork_pb_t_kernel(
         def accumulate(k, i):
             tile_no = k % UNITS * UNIT_TILES + i
             total = acc[:, tile_no, :]
-            adder = nc.vector if (k, i) in ADD_BY_VECTOR else nc.gpsimd
+            adder = nc.vector if k == LAST - 2 and i >= UNIT_TILES // 2 else nc.gpsimd
             adder.tensor_tensor(out=total, in0=total, in1=tiles["product%d" % i, k], op=ALU.add)
             if k // UNITS == VARS - 1:
-                nc.sync.dma_start(out=out[tile_no * P : (tile_no + 1) * P, :], in_=total)
+                nc.scalar.dma_start(out=out[tile_no * P : (tile_no + 1) * P, :], in_=total)
 
         load_hv(0)
         for m in range(3):
@@ -425,7 +441,8 @@ def tile_variableselectionnetwork_pb_t_kernel(
         load_x(0)
         load_hv(2)
         weight_load(3)
-        load_sel(LAST)
+        for k in DIRECT:
+            load_sel(k)
         weight_regroup(0)
         hv_transpose(0, 0)
         hv_transpose(0, 1)
@@ -450,7 +467,8 @@ def tile_variableselectionnetwork_pb_t_kernel(
                 load_hv(step + 3)
             if live(step + 1):
                 load_x(step + 1)
-            load_sel(step)
+            if step not in DIRECT:
+                load_sel(step)
             if step + 4 < 3 * VARS:
                 weight_load(step + 4)
 
@@ -473,6 +491,12 @@ def tile_variableselectionnetwork_pb_t_kernel(
                 weight_quantise(step + 3)
             if live(step + 2):
                 hv_quantise(step + 2)
+            if step == 9:
+                for i in (0, 1):
+                    sel_times_gain(LAST, i)
+            if step == 10:
+                for i in (2, 3):
+                    sel_times_gain(LAST, i)
             if live(step - 1):
                 squares(step - 1)
                 normalise(step - 1)
@@ -485,39 +509,41 @@ def tile_variableselectionnetwork_pb_t_kernel(
                 hv_transpose(step + 3, 0)
                 hv_transpose(step + 3, 1)
             mean(step)
+            if step == 0:
+                for i in range(UNIT_TILES):
+                    sel_times_gain(LAST - 1, i)
             if step == 1:
-                last_sel_shift(0)
-                last_sel_shift(1)
-                last_sel_shift(2)
+                for i in range(UNIT_TILES):
+                    sel_times_shift(LAST - 1, i)
             if step == 2:
-                last_sel_shift(3)
-                last_sel_gain(0)
-                last_sel_gain(1)
-            if step == 3:
-                last_sel_gain(2)
-                last_sel_gain(3)
-            if live(step - 2) and (step - 2 >= UNITS or step - 2 == LAST % UNITS):
+                for i in range(UNIT_TILES):
+                    sel_times_shift(LAST, i)
+            if live(step - 2) and step - 2 > 0:
                 for i in range(UNIT_TILES):
                     accumulate(step - 2, i)
 
         gate_layers(LAST)
-        squares(LAST - 1)
-        normalise(LAST - 1)
         gain_shift(LAST - 2, range(CHUNKS))
         for i in range(UNIT_TILES):
             residual(LAST, i)
-            last_moments(i)
-        last_deviation()
-        for i in range(UNIT_TILES):
-            last_centre(i)
+        mean(LAST)
+        squares(LAST)
+        last_moments()
+        squares(LAST - 1)
+        for i in range(UNIT_TILES // 2):
+            centre(LAST - 1, i)
         for i in range(UNIT_TILES):
             weigh(LAST - 2, i)
-        for i in range(UNIT_TILES):
+        for i in range(UNIT_TILES // 2):
             accumulate(LAST - 2, i)
-        gain_shift(LAST - 1, range(CHUNKS))
+        inverse_deviation(LAST - 1)
+        inverse_deviation(LAST)
         for i in range(UNIT_TILES):
-            weigh(LAST - 1, i)
-        for i in range(UNIT_TILES):
-            last_finish(i)
-        for i in range(UNIT_TILES):
-            accumulate(LAST - 1, i)
+            centre(LAST, i)
+        for i in range(UNIT_TILES // 2, UNIT_TILES):
+            accumulate(LAST - 2, i)
+        for i in range(UNIT_TILES // 2, UNIT_TILES):
+            centre(LAST - 1, i)
+        for k in DIRECT:
+            for i in range(UNIT_TILES):
+                finish(k, i)

from contextlib import ExitStack

import concourse.mybir as mybir
from concourse.masks import make_identity

F32 = mybir.dt.float32
BF16 = mybir.dt.bfloat16
U32 = mybir.dt.uint32
U8 = mybir.dt.uint8
FP8X4 = mybir.dt.float8_e4m3fn_x4
ALU = mybir.AluOpType
ACT = mybir.ActivationFunctionType

P = 128
PACK = 4
BATCH = 1536
VARS = 4
D = 512
CHUNKS = D // P
UNIT_ROWS = 512
UNIT_TILES = UNIT_ROWS // P
UNITS = BATCH // UNIT_ROWS
TOTAL = VARS * UNITS
EPS = 1e-5
EARLY = 3
LAST = TOTAL - 1
LAST_BY_VECTOR = 2
DIRECT = (LAST - 1, LAST)
SCALAR_BANKS, VECTOR_BANKS = 4, 4

FLOPS = 3 * VARS * 2 * BATCH * D * D


def tile_variableselectionnetwork_pb_t_kernel(
    tc, hv, x, sel_w, vW1, vb1, vW4, vb4, vW5, vb5, vlng, vlnb, out
):
    nc = tc.nc
    with ExitStack() as ctx:
        ctx.enter_context(tc.manual_schedule())
        const = ctx.enter_context(tc.tile_pool(name="const", bufs=1))
        wstage = ctx.enter_context(tc.tile_pool(name="wstage", bufs=2))
        wquant = ctx.enter_context(tc.tile_pool(name="wquant", bufs=2))
        loads = ctx.enter_context(tc.tile_pool(name="loads", bufs=4))
        quant = ctx.enter_context(tc.tile_pool(name="quant", bufs=2))
        gate = ctx.enter_context(tc.tile_pool(name="gate", bufs=2))
        norm = ctx.enter_context(tc.tile_pool(name="norm", bufs=2 * UNIT_TILES))
        stat = ctx.enter_context(tc.tile_pool(name="stat", bufs=3))
        psum = ctx.enter_context(tc.psum_pool(name="psum", bufs=SCALAR_BANKS))

        ident_f = const.tile([P, P], F32)
        make_identity(nc, ident_f[:])
        ident_b = const.tile([P, P], BF16)
        make_identity(nc, ident_b[:])
        neg_half = const.tile([P, UNIT_TILES], F32)
        nc.vector.memset(neg_half[:], -0.5)
        unread_sigmoid = const.tile([P, UNIT_TILES], F32)
        nc.scalar.activation(out=unread_sigmoid[:], in_=neg_half[:], func=ACT.Sigmoid)

        vb1_cols = const.tile([P, VARS, CHUNKS], BF16)
        nc.scalar.dma_start(out=vb1_cols[:], in_=vb1.rearrange("n (p c) -> p n c", c=CHUNKS))
        bias_rows = const.tile([P, P], BF16)
        nc.vector.memset(bias_rows[:], 0.0)
        for k, vec in enumerate((vb4, vb5)):
            nc.scalar.dma_start(
                out=bias_rows[k * VARS * CHUNKS : (k + 1) * VARS * CHUNKS, :],
                in_=vec.rearrange("n (c m) -> (n c) m", m=P),
            )
        gs_rows = const.tile([P, D], BF16)
        nc.vector.memset(gs_rows[:], 0.0)
        nc.scalar.dma_start(out=gs_rows[0:VARS, :], in_=vlng)
        nc.scalar.dma_start(out=gs_rows[VARS : 2 * VARS, :], in_=vlnb)

        acc = const.tile([P, BATCH // P, D], F32)

        bias_cols = const.tile([P, 2, VARS, CHUNKS], F32)
        gs_cols = const.tile([P, CHUNKS, 2 * VARS], F32)
        gs_spread = const.tile([P, 2, D], BF16)
        sel_gain = const.tile([P, len(DIRECT) * UNIT_TILES, D], F32)

        tiles = {}

        def live(k):
            return 0 <= k < TOTAL

        def weight_load(m):
            n = m // 3
            raw = wstage.tile([P, PACK, D], BF16, tag="w_raw", bufs=4)
            w = (vW1, vW4, vW5)[m % 3]
            nc.sync.dma_start(out=raw[:], in_=w[n].rearrange("(p t) c -> p t c", t=PACK))
            tiles["w_raw", m] = raw

        def weight_regroup(m):
            raw = tiles["w_raw", m]
            grouped = wstage.tile([P, D, PACK], BF16, tag="w_grp", align_bytes=64)
            tiles["w_grp", m] = grouped
            if m % 3 == 0:
                to = grouped[:].rearrange("p (t m) j -> p t m j", t=PACK)
                fro = raw[:].rearrange("p j (m t) -> p t m j", t=PACK)
                split = PACK // 2
            else:
                to = grouped[:].rearrange("p (c i) j -> p c j i", i=4)
                fro = raw[:].rearrange("p j (c i) -> p c j i", i=4)
                split = D // 4 // 2
            nc.vector.tensor_copy(out=to[:, :split], in_=fro[:, :split])
            nc.scalar.copy(out=to[:, split:], in_=fro[:, split:])

        def weight_quantise(m):
            codes = wquant.tile([P, D], U32, tag="w_codes%d" % (m % 3), align_bytes=64)
            scales = wquant.tile([P, D], U8, tag="w_scales%d" % (m % 3), align_bytes=64)
            nc.vector.quantize_mx(
                out=codes[:].bitcast(FP8X4),
                scales=scales[:],
                in_=tiles["w_grp", m][:].rearrange("p c t -> p (c t)"),
            )
            tiles["w_codes", m] = codes
            tiles["w_scales", m] = scales

        def mx_pass(out_ps, m, c, codes, scales, rows=slice(0, UNIT_ROWS)):
            feats = slice(c * P, (c + 1) * P)
            nc.tensor.matmul_mx(
                out=out_ps,
                lhsT=tiles["w_codes", m][:, feats].bitcast(FP8X4),
                lhsT_scale=tiles["w_scales", m][:, feats],
                rhs=codes[:, rows].bitcast(FP8X4),
                rhs_scale=scales[:, rows],
                start=True,
                stop=True,
            )

        def column_constants():
            bias_ps = psum.tile([P, P], BF16, tag="to_scalar")
            nc.tensor.transpose(bias_ps[:], bias_rows[:], ident_b[:])
            nc.scalar.copy(
                out=bias_cols[:].rearrange("p k n c -> p (k n c)"), in_=bias_ps[:, 0 : 2 * VARS * CHUNKS]
            )
            gs_ps = psum.tile([P, CHUNKS, P], BF16, tag="to_scalar")
            for c in range(CHUNKS):
                nc.tensor.transpose(gs_ps[:, c, :], gs_rows[:, c * P : (c + 1) * P], ident_b[:])
            nc.scalar.copy(out=gs_cols[:], in_=gs_ps[:, :, 0 : 2 * VARS])
            spread_ps = psum.tile([P, 2, D], BF16, tag="to_scalar")
            for v in range(2):
                row = v * VARS + VARS - 1
                nc.tensor.matmul(
                    out=spread_ps[:, v, :],
                    lhsT=ident_b[:, row : row + 1].to_broadcast([P, P]),
                    rhs=gs_rows[:],
                    start=True,
                    stop=True,
                )
            nc.scalar.copy(out=gs_spread[:], in_=spread_ps[:])

        def sel_gain_of(k, i):
            return sel_gain[:, DIRECT.index(k) * UNIT_TILES + i, :]

        def sel_times_gain(k, i):
            engine = nc.vector if k == LAST else nc.gpsimd
            engine.tensor_tensor(
                out=sel_gain_of(k, i), in0=tiles["sel_u", k][:, i, :], in1=gs_spread[:, 0, :], op=ALU.mult
            )

        def sel_times_shift(k, i):
            nc.gpsimd.tensor_tensor(
                out=acc[:, k % UNITS * UNIT_TILES + i, :],
                in0=tiles["sel_u", k][:, i, :],
                in1=gs_spread[:, 1, :],
                op=ALU.mult,
            )

        def unit_rows(dram, k):
            first = (k % UNITS) * UNIT_ROWS
            return dram[first : first + UNIT_ROWS, k // UNITS, :].rearrange("(i p) d -> p i d", p=P)

        def load_hv(k):
            hv_u = loads.tile([P, UNIT_TILES * D], BF16, tag="hv_u", bufs=3)
            nc.sync.dma_start(out=hv_u[:].rearrange("p (i d) -> p i d", i=UNIT_TILES), in_=unit_rows(hv, k))
            tiles["hv_u", k] = hv_u

        def load_x(k):
            x_u = loads.tile([P, UNIT_TILES, D], BF16, tag="x_u", bufs=3)
            nc.sync.dma_start(out=x_u[:], in_=unit_rows(x, k))
            tiles["x_u", k] = x_u

        def load_sel(k):
            direct = k in DIRECT
            sel_u = loads.tile(
                [P, UNIT_TILES, D], BF16, tag="sel_direct" if direct else "sel_u", bufs=len(DIRECT) if direct else 3
            )
            nc.sync.dma_start(out=sel_u[:], in_=unit_rows(sel_w, k))
            tiles["sel_u", k] = sel_u

        def hv_transpose(k, half):
            hv_words = tiles["hv_u", k][:].bitcast(F32)
            if half == 0:
                hv_grp = quant.tile([P, UNIT_ROWS * PACK], BF16, tag="hv_grp", align_bytes=64)
            else:
                hv_grp = tiles["hv_grp", k]
            hv_grp_words = hv_grp[:].bitcast(F32).rearrange("p (b u) -> p b u", u=2)
            if True:
                on_scalar = k < EARLY or (half == 1)
                hv_t = psum.tile(
                    [P, 2, 2 * P],
                    F32,
                    tag="to_scalar" if on_scalar else "to_vector",
                    bufs=SCALAR_BANKS if on_scalar else VECTOR_BANKS,
                )
                for u in range(2):
                    for j in range(2):
                        i = 2 * half + j
                        nc.tensor.transpose(
                            hv_t[:, u, j * P : (j + 1) * P],
                            hv_words[:, i * 2 * P + u : (i + 1) * 2 * P : 2],
                            ident_f[:],
                        )
                to = hv_grp_words[:, half * 2 * P : (half + 1) * 2 * P, :]
                if on_scalar:
                    nc.scalar.copy(out=to, in_=hv_t[:].rearrange("p u b -> p b u"))
                else:
                    nc.vector.tensor_copy(out=to, in_=hv_t[:].rearrange("p u b -> p b u"))
            tiles["hv_grp", k] = hv_grp

        def hv_quantise(k):
            codes = quant.tile([P, UNIT_ROWS], U32, tag="hv_codes", align_bytes=64)
            scales = quant.tile([P, UNIT_ROWS], U8, tag="hv_scales", align_bytes=64)
            nc.vector.quantize_mx(out=codes[:].bitcast(FP8X4), scales=scales[:], in_=tiles["hv_grp", k][:])
            tiles["hv_codes", k] = codes
            tiles["hv_scales", k] = scales

        def first_layer(k, i):
            n = k // UNITS
            if i == 0:
                grouped = quant.tile([P, UNIT_ROWS, PACK], BF16, tag="e1_grp", align_bytes=64)
                tiles["e1_grp", k] = grouped
            grouped = tiles["e1_grp", k]
            rows = slice(i * P, (i + 1) * P)
            e1_ps = psum.tile([P, CHUNKS, P], F32, tag="to_vector", bufs=VECTOR_BANKS)
            for c in range(CHUNKS):
                mx_pass(e1_ps[:, c, :], 3 * n, c, tiles["hv_codes", k], tiles["hv_scales", k], rows)
            nc.vector.tensor_tensor(
                out=grouped[:, rows, :],
                in0=e1_ps[:].rearrange("p c b -> p b c"),
                in1=vb1_cols[:, n, :].unsqueeze(1).to_broadcast([P, P, CHUNKS]),
                op=ALU.add,
            )

        def e1_quantise(k):
            codes = quant.tile([P, UNIT_ROWS], U32, tag="e1_codes", align_bytes=64)
            scales = quant.tile([P, UNIT_ROWS], U8, tag="e1_scales", align_bytes=64)
            nc.vector.quantize_mx(
                out=codes[:].bitcast(FP8X4),
                scales=scales[:],
                in_=tiles["e1_grp", k][:].rearrange("p b t -> p (b t)"),
            )
            tiles["e1_codes", k] = codes
            tiles["e1_scales", k] = scales

        def gate_layers(k):
            n = k // UNITS
            gv_t = gate.tile([P, CHUNKS, UNIT_ROWS], F32, tag="gv_t", bufs=1)
            for c in range(CHUNKS):
                g4_ps = psum.tile([P, UNIT_ROWS], F32, tag="to_scalar")
                mx_pass(g4_ps[:], 3 * n + 1, c, tiles["e1_codes", k], tiles["e1_scales", k])
                g5_ps = psum.tile([P, UNIT_ROWS], F32, tag="to_vector", bufs=VECTOR_BANKS)
                mx_pass(g5_ps[:], 3 * n + 2, c, tiles["e1_codes", k], tiles["e1_scales", k])
                sig = gate.tile([P, UNIT_ROWS], F32, tag="sig", bufs=3)
                nc.scalar.activation(
                    out=sig[:], in_=g4_ps[:], func=ACT.Sigmoid, bias=bias_cols[:, 0, n, c : c + 1], scale=1.0
                )
                nc.vector.scalar_tensor_tensor(
                    out=gv_t[:, c, :],
                    in0=g5_ps[:],
                    scalar=bias_cols[:, 1, n, c : c + 1],
                    in1=sig[:],
                    op0=ALU.add,
                    op1=ALU.mult,
                )
            tiles["gv_t", k] = gv_t

        def by_scalar_from(k):
            return LAST_BY_VECTOR if k == LAST else 0

        def residual(k, i):
            if i == 0:
                row_sum = stat.tile([P, UNIT_TILES], F32, tag="row_sum")
                tiles["row_sum", k] = row_sum
            r_ps = psum.tile([P, D], F32, tag="to_scalar")
            nc.tensor.matmul(out=r_ps[:], lhsT=ident_b[:], rhs=tiles["x_u", k][:, i, :], start=True, stop=False)
            for c in range(CHUNKS):
                nc.tensor.matmul(
                    out=r_ps[:, c * P : (c + 1) * P],
                    lhsT=tiles["gv_t", k][:, c, i * P : (i + 1) * P],
                    rhs=ident_f[:],
                    is_transpose=True,
                    start=False,
                    stop=(c == CHUNKS - 1),
                )
            tiles["r_ps%d" % i, k] = r_ps
            if i >= by_scalar_from(k):
                r = norm.tile([P, D], F32, tag="r")
                nc.scalar.activation(
                    out=r[:], in_=r_ps[:], func=ACT.Identity, accum_out=tiles["row_sum", k][:, i : i + 1]
                )
                tiles["r%d" % i, k] = r

        def last_moments():
            mean_var = stat.tile([P, LAST_BY_VECTOR, 2], F32, tag="mean_var")
            for i in range(LAST_BY_VECTOR):
                moments = stat.tile([P, 6], F32, tag="moments")
                nc.vector.bn_stats(out=moments[:], in_=tiles["r_ps%d" % i, LAST][:])
                nc.vector.bn_aggr(out=mean_var[:, i, :], in_=moments[:])
            tiles["mean_var", LAST] = mean_var
            nc.vector.tensor_scalar(
                out=tiles["var_eps", LAST][:, 0:LAST_BY_VECTOR],
                in0=mean_var[:, :, 1],
                scalar1=EPS,
                scalar2=None,
                op0=ALU.add,
            )

        def inverse_deviation(k):
            rstd = stat.tile([P, UNIT_TILES], F32, tag="rstd")
            nc.gpsimd.tensor_tensor(out=rstd[:], in0=tiles["var_eps", k][:], in1=neg_half[:], op=ALU.pow)
            tiles["rstd", k] = rstd

        def centre(k, i):
            if i == 0:
                z = gate.tile([P, UNIT_TILES, D], F32, tag="z", bufs=2)
                tiles["z", k] = z
            by_scalar = i >= by_scalar_from(k)
            nc.vector.scalar_tensor_tensor(
                out=tiles["z", k][:, i, :],
                in0=tiles[("r_ps%d" if k == LAST else "r%d") % i, k][:],
                scalar=tiles["neg_mean", k][:, i : i + 1] if by_scalar else tiles["mean_var", k][:, i, 0:1],
                in1=sel_gain_of(k, i),
                op0=ALU.add if by_scalar else ALU.subtract,
                op1=ALU.mult,
            )

        def finish(k, i):
            tile_no = k % UNITS * UNIT_TILES + i
            total = acc[:, tile_no, :]
            nc.vector.scalar_tensor_tensor(
                out=total,
                in0=tiles["z", k][:, i, :],
                scalar=tiles["rstd", k][:, i : i + 1],
                in1=total,
                op0=ALU.mult,
                op1=ALU.add,
            )
            nc.sync.dma_start(out=out[tile_no * P : (tile_no + 1) * P, :], in_=total)

        def mean(k):
            neg_mean = stat.tile([P, UNIT_TILES], F32, tag="neg_mean")
            cols = slice(by_scalar_from(k), UNIT_TILES)
            nc.scalar.mul(out=neg_mean[:, cols], in_=tiles["row_sum", k][:, cols], mul=-1.0 / D)
            tiles["neg_mean", k] = neg_mean

        def squares(k):
            sq_sum = stat.tile([P, UNIT_TILES], F32, tag="sq_sum")
            for i in range(by_scalar_from(k), UNIT_TILES):
                sq = norm.tile([P, D], BF16, tag="squares", bufs=4)
                nc.scalar.activation(
                    out=sq[:],
                    in_=tiles["r%d" % i, k][:],
                    func=ACT.Square,
                    bias=tiles["neg_mean", k][:, i : i + 1],
                    scale=1.0,
                    accum_out=sq_sum[:, i : i + 1],
                )
            var_eps = stat.tile([P, UNIT_TILES], F32, tag="var_eps")
            cols = slice(by_scalar_from(k), UNIT_TILES)
            nc.scalar.activation(out=var_eps[:, cols], in_=sq_sum[:, cols], func=ACT.Copy, bias=EPS, scale=1.0 / D)
            tiles["var_eps", k] = var_eps

        def normalise(k):
            for i in range(UNIT_TILES):
                normalise_tile(k, i)

        def normalise_tile(k, i):
            if i == 0:
                rstd = stat.tile([P, UNIT_TILES], F32, tag="rstd")
                nc.gpsimd.tensor_tensor(out=rstd[:], in0=tiles["var_eps", k][:], in1=neg_half[:], op=ALU.pow)
                z = gate.tile([P, UNIT_TILES, D], F32, tag="z", bufs=2)
                tiles["rstd", k] = rstd
                tiles["z", k] = z
            nc.gpsimd.tensor_scalar(
                out=tiles["z", k][:, i, :],
                in0=tiles["r%d" % i, k][:],
                scalar1=tiles["neg_mean", k][:, i : i + 1],
                scalar2=tiles["rstd", k][:, i : i + 1],
                op0=ALU.add,
                op1=ALU.mult,
            )

        def gain_shift(k, chunks):
            n = k // UNITS
            if 0 in chunks:
                y = gate.tile([P, CHUNKS, UNIT_ROWS], F32, tag="y")
                tiles["y", k] = y
            y = tiles["y", k]
            for c in chunks:
                z_ps = psum.tile([P, UNIT_ROWS], F32, tag="to_scalar")
                for i in range(UNIT_TILES):
                    nc.tensor.transpose(
                        z_ps[:, i * P : (i + 1) * P], tiles["z", k][:, i, c * P : (c + 1) * P], ident_f[:]
                    )
                gain = gs_cols[:, c, n : n + 1]
                shift = gs_cols[:, c, VARS + n : VARS + n + 1]
                if k >= LAST - 4 and c == CHUNKS - 1:
                    nc.vector.tensor_scalar(
                        out=y[:, c, :], in0=z_ps[:], scalar1=gain, scalar2=shift, op0=ALU.mult, op1=ALU.add
                    )
                else:
                    nc.scalar.activation(out=y[:, c, :], in_=z_ps[:], func=ACT.Identity, bias=shift, scale=gain)

        def weigh(k, i):
            y_ps = psum.tile([P, D], F32, tag="to_vector", bufs=VECTOR_BANKS)
            for c in range(CHUNKS):
                nc.tensor.transpose(
                    y_ps[:, c * P : (c + 1) * P], tiles["y", k][:, c, i * P : (i + 1) * P], ident_f[:]
                )
            if k == 0:
                product = acc[:, k % UNITS * UNIT_TILES + i, :]
            else:
                product_tile = norm.tile([P, D], F32, tag="product", bufs=6)
                product = product_tile[:]
            nc.vector.tensor_tensor(out=product, in0=y_ps[:], in1=tiles["sel_u", k][:, i, :], op=ALU.mult)
            tiles["product%d" % i, k] = product

        def accumulate(k, i):
            tile_no = k % UNITS * UNIT_TILES + i
            total = acc[:, tile_no, :]
            adder = nc.vector if k == LAST - 2 and i >= UNIT_TILES // 2 else nc.gpsimd
            adder.tensor_tensor(out=total, in0=total, in1=tiles["product%d" % i, k], op=ALU.add)
            if k // UNITS == VARS - 1:
                nc.scalar.dma_start(out=out[tile_no * P : (tile_no + 1) * P, :], in_=total)

        load_hv(0)
        for m in range(3):
            weight_load(m)
        load_hv(1)
        load_x(0)
        load_hv(2)
        weight_load(3)
        for k in DIRECT:
            load_sel(k)
        weight_regroup(0)
        hv_transpose(0, 0)
        hv_transpose(0, 1)
        weight_quantise(0)
        hv_quantise(0)
        weight_regroup(1)
        weight_regroup(2)
        for i in range(UNIT_TILES):
            first_layer(0, i)
        hv_transpose(1, 0)
        hv_transpose(1, 1)
        column_constants()
        hv_transpose(2, 0)
        hv_transpose(2, 1)
        weight_quantise(1)
        weight_quantise(2)
        e1_quantise(0)
        hv_quantise(1)

        for step in range(LAST):
            if live(step + 3):
                load_hv(step + 3)
            if live(step + 1):
                load_x(step + 1)
            if step not in DIRECT:
                load_sel(step)
            if step + 4 < 3 * VARS:
                weight_load(step + 4)

            if live(step):
                gate_layers(step)
            if live(step - 2):
                gain_shift(step - 2, (0, 1))
            if live(step + 1):
                first_layer(step + 1, 0)
            if live(step - 2):
                gain_shift(step - 2, (2, 3))
            if live(step + 1):
                for i in range(1, UNIT_TILES):
                    first_layer(step + 1, i)
            if step + 3 < 3 * VARS:
                weight_regroup(step + 3)
            if live(step + 1):
                e1_quantise(step + 1)
            if step + 3 < 3 * VARS:
                weight_quantise(step + 3)
            if live(step + 2):
                hv_quantise(step + 2)
            if step == 9:
                for i in (0, 1):
                    sel_times_gain(LAST, i)
            if step == 10:
                for i in (2, 3):
                    sel_times_gain(LAST, i)
            if live(step - 1):
                squares(step - 1)
                normalise(step - 1)
            for i in range(UNIT_TILES):
                if live(step - 2):
                    weigh(step - 2, i)
                if live(step):
                    residual(step, i)
            if live(step + 3):
                hv_transpose(step + 3, 0)
                hv_transpose(step + 3, 1)
            mean(step)
            if step == 0:
                for i in range(UNIT_TILES):
                    sel_times_gain(LAST - 1, i)
            if step == 1:
                for i in range(UNIT_TILES):
                    sel_times_shift(LAST - 1, i)
            if step == 2:
                for i in range(UNIT_TILES):
                    sel_times_shift(LAST, i)
            if live(step - 2) and step - 2 > 0:
                for i in range(UNIT_TILES):
                    accumulate(step - 2, i)

        gate_layers(LAST)
        gain_shift(LAST - 2, range(CHUNKS))
        for i in range(UNIT_TILES):
            residual(LAST, i)
        mean(LAST)
        squares(LAST)
        last_moments()
        squares(LAST - 1)
        for i in range(UNIT_TILES // 2):
            centre(LAST - 1, i)
        for i in range(UNIT_TILES):
            weigh(LAST - 2, i)
        for i in range(UNIT_TILES // 2):
            accumulate(LAST - 2, i)
        inverse_deviation(LAST - 1)
        inverse_deviation(LAST)
        for i in range(UNIT_TILES):
            centre(LAST, i)
        for i in range(UNIT_TILES // 2, UNIT_TILES):
            accumulate(LAST - 2, i)
        for i in range(UNIT_TILES // 2, UNIT_TILES):
            centre(LAST - 1, i)
        for k in DIRECT:
            for i in range(UNIT_TILES):
                finish(k, i)
